import numpy as np
import ml_dtypes


BF16 = ml_dtypes.bfloat16


def bf(x):
    return np.asarray(x, np.float32).astype(BF16)


def f64(x):
    return np.asarray(x).astype(np.float64)


E2M1 = np.array([0.0, 0.5, 1.0, 1.5, 2.0, 3.0, 4.0, 6.0, -0.0, -0.5, -1.0, -1.5, -2.0, -3.0, -4.0, -6.0])


def pack_weight(w, fmt):
    k, n = w.shape
    w = f64(bf(w)).reshape(k // 32, 32, n)
    amax = np.abs(w).max(1)
    if fmt == "e4m3":
        byte = np.frexp(amax)[1] - 1 + 127 - 7
    else:
        mant, ex = np.frexp(amax / 6.0)
        byte = np.where(mant > 0.5, ex, ex - 1) + 127
    byte = np.clip(np.where(amax > 0, byte, 1), 1, 254)
    scaled = (w * np.exp2(127.0 - byte)[:, None, :]).reshape(k, n).astype(np.float32)
    by_word = np.ascontiguousarray(scaled.reshape(k // 512, 128, 4, n).transpose(0, 1, 3, 2))
    if fmt == "e4m3":
        words = by_word.astype(ml_dtypes.float8_e4m3fn).view(np.uint8)
    else:
        c = by_word.astype(ml_dtypes.float4_e2m1fn).view(np.uint8) & 0xF
        words = c[..., 0::2] | (c[..., 1::2] << 4)
    return np.ascontiguousarray(words), np.ascontiguousarray(byte.astype(np.uint8).reshape(k // 512, 16, n))


def unpack_weight(words, scales, fmt):
    g, p, n, _ = words.shape
    if fmt == "e4m3":
        vals = np.ascontiguousarray(words).view(ml_dtypes.float8_e4m3fn).astype(np.float64)
    else:
        nib = np.empty((g, p, n, 4), np.uint8)
        nib[..., 0::2] = words & 0xF
        nib[..., 1::2] = words >> 4
        vals = E2M1[nib]
    vals = vals * np.repeat(np.exp2(scales.astype(np.float64) - 127.0), 8, axis=1)[..., None]
    return vals.transpose(0, 1, 3, 2).reshape(g * 512, n)

def pack4(w):
    words, scales = pack_weight(w, "e2m1")
    return words.reshape(words.shape[0], 128, -1), scales


def unpack4(words, scales):
    return unpack_weight(words.reshape(words.shape[0], 128, -1, 2), scales, "e2m1")


def kspread(k):
    return np.exp2(np.repeat(np.random.randint(-6, 7, k // 32), 32).astype(np.float64))


T, D, E = 4096, 4096, 768


def setup_inputs():
    s = kspread(D)
    hidden_states = np.random.standard_normal((T, D)) * s
    hidden_states_words, hidden_states_scales = pack4(np.ascontiguousarray(hidden_states.T))
    weight = np.random.standard_normal((E, D)) * 1.0 / np.sqrt(D) / s[None, :]
    words, scales = pack4(np.ascontiguousarray(weight.T))
    return {"hidden_states_words": hidden_states_words,
            "hidden_states_scales": hidden_states_scales,
            "weight_words": words,
            "weight_scales": scales}


def reference(hidden_states_words, hidden_states_scales, weight_words, weight_scales):
    logits = unpack4(hidden_states_words, hidden_states_scales).T @ unpack4(weight_words, weight_scales)
    return logits

@@ -1,0 +1,150 @@
+from contextlib import ExitStack
+
+import concourse.mybir as mybir
+
+T, D, E = 4096, 4096, 768
+FLOPS = 2 * T * D * E
+
+F32 = mybir.dt.float32
+BF16 = mybir.dt.bfloat16
+I32 = mybir.dt.int32
+U8 = mybir.dt.uint8
+FP4X4 = mybir.dt.float4_e2m1fn_x4
+
+P = 128
+PASSES = D // 512
+BIG = 512
+SMALL = E - BIG
+WORD = 2
+
+PIECES = ((0, 512), (512, 1024), (1024, 2048), (2048, 4096))
+FIRST_BLOCKS = PIECES[0][1] // P
+
+W_RUNS = ((0, 4), (4, 8))
+X_RUNS = ((0, 3), (3, 8))
+EACH = tuple((g, g + 1) for g in range(PASSES))
+ALL = ((0, PASSES),)
+
+WARM_UPS = 36
+
+
+def tile_longcatrouter_kernel(tc, x_words, x_scales, w_words, w_scales, out):
+    nc = tc.nc
+    with ExitStack() as ctx:
+        keep = ctx.enter_context(tc.tile_pool(name="keep", bufs=1))
+        results = ctx.enter_context(tc.tile_pool(name="results", bufs=16))
+        psum = ctx.enter_context(tc.psum_pool(name="psum", bufs=1))
+        ctx.enter_context(tc.manual_schedule())
+
+        def tiles(name, runs, width):
+            return [keep.tile([P, b - a, width], U8, align_bytes=256, name="%s_%d" % (name, a)) for a, b in runs]
+
+        def of_pass(run_tiles, runs, g):
+            i = [a <= g < b for a, b in runs].index(True)
+            return run_tiles[i], g - runs[i][0]
+
+        w_codes = tiles("w_codes", EACH, WORD * E)
+        w_planes = tiles("w_planes", W_RUNS, E)
+        x_code_runs = [EACH] + [ALL] * (len(PIECES) - 1)
+        x_plane_runs = [X_RUNS] + [ALL] * (len(PIECES) - 1)
+        x_codes = [tiles("x_codes%d" % i, x_code_runs[i], WORD * (t1 - t0)) for i, (t0, t1) in enumerate(PIECES)]
+        x_planes = [tiles("x_planes%d" % i, x_plane_runs[i], t1 - t0) for i, (t0, t1) in enumerate(PIECES)]
+
+        warm = keep.tile([P, P], BF16, name="warm")
+        nc.gpsimd.memset(warm[:], 0.0)
+
+        def zero(plane):
+            nc.vector.memset(plane[:].bitcast(I32), 0)
+
+        for plane in (w_planes[0], x_planes[0][0], x_planes[0][1], w_planes[1]):
+            zero(plane)
+        for i in range(1, len(PIECES)):
+            zero(x_planes[i][0])
+
+        def load_codes(tile, words, a, b, c0, c1):
+            src = words[a:b, :, WORD * c0 : WORD * c1].rearrange("g p n -> p g n")
+            nc.sync.dma_start(out=tile[:].bitcast(I32), in_=src.bitcast(I32))
+
+        def load_scales(plane, scales, a, b, c0, c1):
+            for r in range(4):
+                src = scales[a:b, r:16:4, c0:c1].rearrange("g q n -> q g n")
+                nc.sync.dma_start(out=plane[r:P:32, :, :].bitcast(I32), in_=src.bitcast(I32))
+
+        def load_piece(i):
+            t0, t1 = PIECES[i]
+            load_codes(x_codes[i][0], x_words, 0, PASSES, t0, t1)
+            load_scales(x_planes[i][0], x_scales, 0, PASSES, t0, t1)
+
+        def load_codes_of_pass(g):
+            load_codes(x_codes[0][g], x_words, g, g + 1, *PIECES[0])
+            load_codes(w_codes[g], w_words, g, g + 1, 0, E)
+
+        load_codes_of_pass(0)
+        for g in range(PASSES):
+            for plane, (a, b) in zip(w_planes, W_RUNS):
+                if a == g:
+                    load_scales(plane, w_scales, a, b, 0, E)
+            for plane, (a, b) in zip(x_planes[0], X_RUNS):
+                if a == g:
+                    load_scales(plane, x_scales, a, b, *PIECES[0])
+            if g > 0:
+                load_codes_of_pass(g)
+        load_piece(1)
+        load_piece(2)
+
+        def bank(i):
+            return psum.tile([P, BIG], F32, tag="bank%d" % i, name="bank%d" % i)
+
+        warm_bank = bank(7)
+        for i in range(WARM_UPS):
+            nc.tensor.matmul(warm_bank[:, 0:P], warm[:], warm[:], start=True, stop=True)
+
+        def multiply(acc, block, g, e0, e1):
+            tok = P * block
+            i = [t0 <= tok < t1 for t0, t1 in PIECES].index(True)
+            col = tok - PIECES[i][0]
+            xc, xc_g = of_pass(x_codes[i], x_code_runs[i], g)
+            xp, xp_g = of_pass(x_planes[i], x_plane_runs[i], g)
+            wp, wp_g = of_pass(w_planes, W_RUNS, g)
+            nc.tensor.matmul_mx(
+                out=acc[:, 0 : e1 - e0],
+                lhsT=xc[:, xc_g, WORD * col : WORD * (col + P)].bitcast(FP4X4),
+                lhsT_scale=xp[:, xp_g, col : col + P],
+                rhs=w_codes[g][:, 0, WORD * e0 : WORD * e1].bitcast(FP4X4),
+                rhs_scale=wp[:, wp_g, e0:e1],
+                start=(g == 0),
+                stop=(g == PASSES - 1),
+            )
+
+        last = T // P - 1
+
+        def store(big, small, block):
+            logits = results.tile([P, E], F32, name="logits")
+            rows = out[P * block : P * (block + 1), :]
+            nc.scalar.copy(out=logits[:, 0:BIG], in_=big[:])
+            nc.vector.tensor_copy(out=logits[:, BIG:E], in_=small[:, 0:SMALL])
+            if block < last:
+                nc.sync.dma_start(out=rows, in_=logits[:])
+            else:
+                nc.sync.dma_start(out=rows[:, 0:BIG], in_=logits[:, 0:BIG])
+                nc.sync.dma_start(out=rows[:, BIG:E], in_=logits[:, BIG:E])
+
+        banks = [(bank(2 * block), bank(2 * block + 1)) for block in range(FIRST_BLOCKS)]
+        for g in range(PASSES):
+            for block in range(FIRST_BLOCKS):
+                big, small = banks[block]
+                multiply(big, block, g, 0, BIG)
+                multiply(small, block, g, BIG, E)
+        for block in range(FIRST_BLOCKS):
+            store(*banks[block], block)
+
+        load_piece(3)
+
+        for block in range(FIRST_BLOCKS, last + 1):
+            j = block % FIRST_BLOCKS
+            big, small = bank(2 * j), bank(2 * j + 1)
+            for g in range(PASSES):
+                multiply(big, block, g, 0, BIG)
+            for g in range(PASSES):
+                multiply(small, block, g, BIG, E)
+            store(big, small, block)

@@ -6,7 +6,6 @@ T, D, E = 4096, 4096, 768
 FLOPS = 2 * T * D * E
 
 F32 = mybir.dt.float32
-BF16 = mybir.dt.bfloat16
 I32 = mybir.dt.int32
 U8 = mybir.dt.uint8
 FP4X4 = mybir.dt.float4_e2m1fn_x4
@@ -18,14 +17,16 @@ SMALL = E - BIG
 WORD = 2
 
 PIECES = ((0, 512), (512, 1024), (1024, 2048), (2048, 4096))
-FIRST_BLOCKS = PIECES[0][1] // P
+FIRST = PIECES[0][1]
+FIRST_BLOCKS = FIRST // P
+START = 2 * P
 
 W_RUNS = ((0, 4), (4, 8))
 X_RUNS = ((0, 3), (3, 8))
 EACH = tuple((g, g + 1) for g in range(PASSES))
 ALL = ((0, PASSES),)
 
-WARM_UPS = 36
+WARM_UPS = 4
 
 
 def tile_longcatrouter_kernel(tc, x_words, x_scales, w_words, w_scales, out):
@@ -36,82 +37,77 @@ def tile_longcatrouter_kernel(tc, x_words, x_scales, w_words, w_scales, out):
         psum = ctx.enter_context(tc.psum_pool(name="psum", bufs=1))
         ctx.enter_context(tc.manual_schedule())
 
-        def tiles(name, runs, width):
-            return [keep.tile([P, b - a, width], U8, align_bytes=256, name="%s_%d" % (name, a)) for a, b in runs]
+        def load(name, a, b, c0, c1, width):
+            shape = [P, b - a, width * (c1 - c0)]
+            return keep.tile(shape, U8, align_bytes=256, name="%s_%d_%d" % (name, a, c0)), a, b, c0, c1
 
-        def of_pass(run_tiles, runs, g):
-            i = [a <= g < b for a, b in runs].index(True)
-            return run_tiles[i], g - runs[i][0]
+        def operand(loads, g, c0, c1, width):
+            tile, a, b, t0, t1 = [x for x in loads if x[1] <= g < x[2] and x[3] <= c0 < x[4]][0]
+            return tile[:, g - a, width * (c0 - t0) : width * (c1 - t0)]
 
-        w_codes = tiles("w_codes", EACH, WORD * E)
-        w_planes = tiles("w_planes", W_RUNS, E)
-        x_code_runs = [EACH] + [ALL] * (len(PIECES) - 1)
-        x_plane_runs = [X_RUNS] + [ALL] * (len(PIECES) - 1)
-        x_codes = [tiles("x_codes%d" % i, x_code_runs[i], WORD * (t1 - t0)) for i, (t0, t1) in enumerate(PIECES)]
-        x_planes = [tiles("x_planes%d" % i, x_plane_runs[i], t1 - t0) for i, (t0, t1) in enumerate(PIECES)]
+        w_start = [load("w_codes", 0, 1, c0, c1, WORD) for c0, c1 in ((0, BIG), (BIG, E))]
+        x_start = [load("x_codes", 0, 1, c0, c1, WORD) for c0, c1 in ((0, START), (START, FIRST))]
+        w_codes = [load("w_codes", a, b, 0, E, WORD) for a, b in EACH[1:]]
+        x_codes = [load("x_codes", a, b, 0, FIRST, WORD) for a, b in EACH[1:]]
+        w_planes = [load("w_planes", a, b, 0, E, 1) for a, b in W_RUNS]
+        x_planes = [load("x_planes", a, b, 0, FIRST, 1) for a, b in X_RUNS]
+        x_codes_later = [load("x_codes", 0, PASSES, t0, t1, WORD) for t0, t1 in PIECES[1:]]
+        x_planes_later = [load("x_planes", 0, PASSES, t0, t1, 1) for t0, t1 in PIECES[1:]]
 
-        warm = keep.tile([P, P], BF16, name="warm")
-        nc.gpsimd.memset(warm[:], 0.0)
+        def zero(tile):
+            nc.vector.memset(tile[:].bitcast(I32), 0)
 
-        def zero(plane):
-            nc.vector.memset(plane[:].bitcast(I32), 0)
+        warm = keep.tile([P, SMALL], F32, name="warm")
+        zero(warm)
+        for plane in [w_planes[0], x_planes[0], x_planes[1], w_planes[1]] + x_planes_later:
+            zero(plane[0])
 
-        for plane in (w_planes[0], x_planes[0][0], x_planes[0][1], w_planes[1]):
-            zero(plane)
-        for i in range(1, len(PIECES)):
-            zero(x_planes[i][0])
-
-        def load_codes(tile, words, a, b, c0, c1):
+        def load_codes(codes, words):
+            tile, a, b, c0, c1 = codes
             src = words[a:b, :, WORD * c0 : WORD * c1].rearrange("g p n -> p g n")
             nc.sync.dma_start(out=tile[:].bitcast(I32), in_=src.bitcast(I32))
 
-        def load_scales(plane, scales, a, b, c0, c1):
+        def load_scales(plane, scales):
+            tile, a, b, c0, c1 = plane
             for r in range(4):
                 src = scales[a:b, r:16:4, c0:c1].rearrange("g q n -> q g n")
-                nc.sync.dma_start(out=plane[r:P:32, :, :].bitcast(I32), in_=src.bitcast(I32))
+                nc.sync.dma_start(out=tile[r:P:32, :, :].bitcast(I32), in_=src.bitcast(I32))
 
         def load_piece(i):
-            t0, t1 = PIECES[i]
-            load_codes(x_codes[i][0], x_words, 0, PASSES, t0, t1)
-            load_scales(x_planes[i][0], x_scales, 0, PASSES, t0, t1)
+            load_codes(x_codes_later[i], x_words)
+            load_scales(x_planes_later[i], x_scales)
 
-        def load_codes_of_pass(g):
-            load_codes(x_codes[0][g], x_words, g, g + 1, *PIECES[0])
-            load_codes(w_codes[g], w_words, g, g + 1, 0, E)
-
-        load_codes_of_pass(0)
-        for g in range(PASSES):
-            for plane, (a, b) in zip(w_planes, W_RUNS):
-                if a == g:
-                    load_scales(plane, w_scales, a, b, 0, E)
-            for plane, (a, b) in zip(x_planes[0], X_RUNS):
-                if a == g:
-                    load_scales(plane, x_scales, a, b, *PIECES[0])
-            if g > 0:
-                load_codes_of_pass(g)
+        load_codes(x_start[0], x_words)
+        load_codes(w_start[0], w_words)
+        load_scales(w_planes[0], w_scales)
+        load_scales(x_planes[0], x_scales)
+        load_codes(x_start[1], x_words)
+        load_codes(w_start[1], w_words)
+        for g in range(1, PASSES):
+            for planes, scales in ((w_planes, w_scales), (x_planes, x_scales)):
+                for plane in planes:
+                    if plane[1] == g:
+                        load_scales(plane, scales)
+            load_codes(x_codes[g - 1], x_words)
+            load_codes(w_codes[g - 1], w_words)
+        load_piece(0)
         load_piece(1)
-        load_piece(2)
 
         def bank(i):
             return psum.tile([P, BIG], F32, tag="bank%d" % i, name="bank%d" % i)
 
         warm_bank = bank(7)
         for i in range(WARM_UPS):
-            nc.tensor.matmul(warm_bank[:, 0:P], warm[:], warm[:], start=True, stop=True)
+            nc.tensor.matmul(warm_bank[:, 0:SMALL], warm[:, 0:P], warm[:], start=True, stop=True)
 
         def multiply(acc, block, g, e0, e1):
-            tok = P * block
-            i = [t0 <= tok < t1 for t0, t1 in PIECES].index(True)
-            col = tok - PIECES[i][0]
-            xc, xc_g = of_pass(x_codes[i], x_code_runs[i], g)
-            xp, xp_g = of_pass(x_planes[i], x_plane_runs[i], g)
-            wp, wp_g = of_pass(w_planes, W_RUNS, g)
+            t0, t1 = P * block, P * (block + 1)
             nc.tensor.matmul_mx(
                 out=acc[:, 0 : e1 - e0],
-                lhsT=xc[:, xc_g, WORD * col : WORD * (col + P)].bitcast(FP4X4),
-                lhsT_scale=xp[:, xp_g, col : col + P],
-                rhs=w_codes[g][:, 0, WORD * e0 : WORD * e1].bitcast(FP4X4),
-                rhs_scale=wp[:, wp_g, e0:e1],
+                lhsT=operand(x_start + x_codes + x_codes_later, g, t0, t1, WORD).bitcast(FP4X4),
+                lhsT_scale=operand(x_planes + x_planes_later, g, t0, t1, 1),
+                rhs=operand(w_start + w_codes, g, e0, e1, WORD).bitcast(FP4X4),
+                rhs_scale=operand(w_planes, g, e0, e1, 1),
                 start=(g == 0),
                 stop=(g == PASSES - 1),
             )
@@ -132,13 +128,13 @@ def tile_longcatrouter_kernel(tc, x_words, x_scales, w_words, w_scales, out):
         banks = [(bank(2 * block), bank(2 * block + 1)) for block in range(FIRST_BLOCKS)]
         for g in range(PASSES):
             for block in range(FIRST_BLOCKS):
-                big, small = banks[block]
-                multiply(big, block, g, 0, BIG)
-                multiply(small, block, g, BIG, E)
+                multiply(banks[block][0], block, g, 0, BIG)
+            for block in range(FIRST_BLOCKS):
+                multiply(banks[block][1], block, g, BIG, E)
         for block in range(FIRST_BLOCKS):
             store(*banks[block], block)
 
-        load_piece(3)
+        load_piece(2)
 
         for block in range(FIRST_BLOCKS, last + 1):
             j = block % FIRST_BLOCKS

@@ -12,77 +12,84 @@ FP4X4 = mybir.dt.float4_e2m1fn_x4
 
 P = 128
 PASSES = D // 512
-BIG = 512
-SMALL = E - BIG
+BANKS = 8
+WIDE = 512
+NARROW = E - WIDE
 WORD = 2
 
-PIECES = ((0, 512), (512, 1024), (1024, 2048), (2048, 4096))
-FIRST = PIECES[0][1]
-FIRST_BLOCKS = FIRST // P
+FIRST_TILES = BANKS // 2
+FIRST = FIRST_TILES * P
+LATER_PIECES = ((FIRST, 2 * FIRST), (2 * FIRST, 4 * FIRST), (4 * FIRST, T))
 START = 2 * P
 
-W_RUNS = ((0, 4), (4, 8))
-X_RUNS = ((0, 3), (3, 8))
-EACH = tuple((g, g + 1) for g in range(PASSES))
-ALL = ((0, PASSES),)
+W_SCALE_RUNS = ((0, 2), (2, 5), (5, 8))
+X_SCALE_RUNS = ((0, 3), (3, 8))
+LATER_CODE_RUNS = (((0, PASSES // 2), (PASSES // 2, PASSES)), ((0, PASSES),), ((0, PASSES),))
 
-WARM_UPS = 4
+WARM_UPS = 3
+RESULT_TILES = 16
 
 
 def tile_longcatrouter_kernel(tc, x_words, x_scales, w_words, w_scales, out):
     nc = tc.nc
     with ExitStack() as ctx:
         keep = ctx.enter_context(tc.tile_pool(name="keep", bufs=1))
-        results = ctx.enter_context(tc.tile_pool(name="results", bufs=16))
+        results = ctx.enter_context(tc.tile_pool(name="results", bufs=RESULT_TILES))
         psum = ctx.enter_context(tc.psum_pool(name="psum", bufs=1))
         ctx.enter_context(tc.manual_schedule())
 
-        def load(name, a, b, c0, c1, width):
-            shape = [P, b - a, width * (c1 - c0)]
-            return keep.tile(shape, U8, align_bytes=256, name="%s_%d_%d" % (name, a, c0)), a, b, c0, c1
+        def part(name, g0, g1, c0, c1, width):
+            shape = [P, g1 - g0, width * (c1 - c0)]
+            return keep.tile(shape, U8, align_bytes=256, name="%s_%d_%d" % (name, g0, c0)), g0, g1, c0, c1
 
-        def operand(loads, g, c0, c1, width):
-            tile, a, b, t0, t1 = [x for x in loads if x[1] <= g < x[2] and x[3] <= c0 < x[4]][0]
-            return tile[:, g - a, width * (c0 - t0) : width * (c1 - t0)]
+        def operand(parts, g, c0, c1, width):
+            tile, g0, g1, first, end = [x for x in parts if x[1] <= g < x[2] and x[3] <= c0 < x[4]][0]
+            return tile[:, g - g0, width * (c0 - first) : width * (c1 - first)]
 
-        w_start = [load("w_codes", 0, 1, c0, c1, WORD) for c0, c1 in ((0, BIG), (BIG, E))]
-        x_start = [load("x_codes", 0, 1, c0, c1, WORD) for c0, c1 in ((0, START), (START, FIRST))]
-        w_codes = [load("w_codes", a, b, 0, E, WORD) for a, b in EACH[1:]]
-        x_codes = [load("x_codes", a, b, 0, FIRST, WORD) for a, b in EACH[1:]]
-        w_planes = [load("w_planes", a, b, 0, E, 1) for a, b in W_RUNS]
-        x_planes = [load("x_planes", a, b, 0, FIRST, 1) for a, b in X_RUNS]
-        x_codes_later = [load("x_codes", 0, PASSES, t0, t1, WORD) for t0, t1 in PIECES[1:]]
-        x_planes_later = [load("x_planes", 0, PASSES, t0, t1, 1) for t0, t1 in PIECES[1:]]
+        w_codes_0 = [part("w_codes", 0, 1, e0, e1, WORD) for e0, e1 in ((0, WIDE), (WIDE, E))]
+        x_codes_0 = [part("x_codes", 0, 1, t0, t1, WORD) for t0, t1 in ((0, START), (START, FIRST))]
+        w_codes = [part("w_codes", g, g + 1, 0, E, WORD) for g in range(1, PASSES)]
+        x_codes = [part("x_codes", g, g + 1, 0, FIRST, WORD) for g in range(1, PASSES)]
+        w_planes = [part("w_planes", g0, g1, 0, E, 1) for g0, g1 in W_SCALE_RUNS]
+        x_planes = [part("x_planes", g0, g1, 0, FIRST, 1) for g0, g1 in X_SCALE_RUNS]
+        later_codes = [
+            [part("x_codes", g0, g1, t0, t1, WORD) for g0, g1 in runs]
+            for (t0, t1), runs in zip(LATER_PIECES, LATER_CODE_RUNS)
+        ]
+        later_planes = [part("x_planes", 0, PASSES, t0, t1, 1) for t0, t1 in LATER_PIECES]
+        all_x_codes = x_codes_0 + x_codes + sum(later_codes, [])
 
         def zero(tile):
             nc.vector.memset(tile[:].bitcast(I32), 0)
 
-        warm = keep.tile([P, SMALL], F32, name="warm")
+        warm = keep.tile([P, NARROW], F32, name="warm")
         zero(warm)
-        for plane in [w_planes[0], x_planes[0], x_planes[1], w_planes[1]] + x_planes_later:
+        for plane in sorted(w_planes + x_planes, key=lambda x: x[1]) + later_planes:
             zero(plane[0])
 
         def load_codes(codes, words):
-            tile, a, b, c0, c1 = codes
-            src = words[a:b, :, WORD * c0 : WORD * c1].rearrange("g p n -> p g n")
+            tile, g0, g1, c0, c1 = codes
+            src = words[g0:g1, :, WORD * c0 : WORD * c1].rearrange("g p n -> p g n")
             nc.sync.dma_start(out=tile[:].bitcast(I32), in_=src.bitcast(I32))
 
         def load_scales(plane, scales):
-            tile, a, b, c0, c1 = plane
+            tile, g0, g1, c0, c1 = plane
             for r in range(4):
-                src = scales[a:b, r:16:4, c0:c1].rearrange("g q n -> q g n")
+                src = scales[g0:g1, r:16:4, c0:c1].rearrange("g q n -> q g n")
                 nc.sync.dma_start(out=tile[r:P:32, :, :].bitcast(I32), in_=src.bitcast(I32))
 
         def load_piece(i):
-            load_codes(x_codes_later[i], x_words)
-            load_scales(x_planes_later[i], x_scales)
+            load_codes(later_codes[i][0], x_words)
+            load_scales(later_planes[i], x_scales)
+            for codes in later_codes[i][1:]:
+                load_codes(codes, x_words)
 
-        load_codes(x_start[0], x_words)
-        load_codes(w_start[0], w_words)
+        load_codes(x_codes_0[0], x_words)
+        load_codes(w_codes_0[0], w_words)
         load_scales(w_planes[0], w_scales)
         load_scales(x_planes[0], x_scales)
-        load_codes(x_start[1], x_words)
-        load_codes(w_start[1], w_words)
+        load_codes(x_codes_0[1], x_words)
+        load_codes(w_codes_0[1], w_words)
         for g in range(1, PASSES):
             for planes, scales in ((w_planes, w_scales), (x_planes, x_scales)):
                 for plane in planes:
@@ -94,19 +101,19 @@ def tile_longcatrouter_kernel(tc, x_words, x_scales, w_words, w_scales, out):
         load_piece(1)
 
         def bank(i):
-            return psum.tile([P, BIG], F32, tag="bank%d" % i, name="bank%d" % i)
+            return psum.tile([P, WIDE], F32, tag="bank%d" % i, name="bank%d" % i)
 
-        warm_bank = bank(7)
+        warm_bank = bank(BANKS - 1)
         for i in range(WARM_UPS):
-            nc.tensor.matmul(warm_bank[:, 0:SMALL], warm[:, 0:P], warm[:], start=True, stop=True)
+            nc.tensor.matmul(warm_bank[:, 0:NARROW], warm[:, 0:P], warm[:], start=True, stop=True)
 
-        def multiply(acc, block, g, e0, e1):
-            t0, t1 = P * block, P * (block + 1)
+        def multiply(acc, j, g, e0, e1):
+            t0, t1 = P * j, P * (j + 1)
             nc.tensor.matmul_mx(
                 out=acc[:, 0 : e1 - e0],
-                lhsT=operand(x_start + x_codes + x_codes_later, g, t0, t1, WORD).bitcast(FP4X4),
-                lhsT_scale=operand(x_planes + x_planes_later, g, t0, t1, 1),
-                rhs=operand(w_start + w_codes, g, e0, e1, WORD).bitcast(FP4X4),
+                lhsT=operand(all_x_codes, g, t0, t1, WORD).bitcast(FP4X4),
+                lhsT_scale=operand(x_planes + later_planes, g, t0, t1, 1),
+                rhs=operand(w_codes_0 + w_codes, g, e0, e1, WORD).bitcast(FP4X4),
                 rhs_scale=operand(w_planes, g, e0, e1, 1),
                 start=(g == 0),
                 stop=(g == PASSES - 1),
@@ -114,33 +121,37 @@ def tile_longcatrouter_kernel(tc, x_words, x_scales, w_words, w_scales, out):
 
         last = T // P - 1
 
-        def store(big, small, block):
+        def store(wide, narrow, j):
             logits = results.tile([P, E], F32, name="logits")
-            rows = out[P * block : P * (block + 1), :]
-            nc.scalar.copy(out=logits[:, 0:BIG], in_=big[:])
-            nc.vector.tensor_copy(out=logits[:, BIG:E], in_=small[:, 0:SMALL])
-            if block < last:
+            rows = out[P * j : P * (j + 1), :]
+            nc.scalar.copy(out=logits[:, 0:WIDE], in_=wide[:])
+            if j < last:
+                nc.vector.tensor_copy(out=logits[:, WIDE:E], in_=narrow[:, 0:NARROW])
                 nc.sync.dma_start(out=rows, in_=logits[:])
             else:
-                nc.sync.dma_start(out=rows[:, 0:BIG], in_=logits[:, 0:BIG])
-                nc.sync.dma_start(out=rows[:, BIG:E], in_=logits[:, BIG:E])
+                nc.sync.dma_start(out=rows[:, 0:WIDE], in_=logits[:, 0:WIDE])
+                half = NARROW // 2
+                for c0 in (0, half):
+                    e0, e1 = WIDE + c0, WIDE + c0 + half
+                    nc.vector.tensor_copy(out=logits[:, e0:e1], in_=narrow[:, c0 : c0 + half])
+                    nc.sync.dma_start(out=rows[:, e0:e1], in_=logits[:, e0:e1])
 
-        banks = [(bank(2 * block), bank(2 * block + 1)) for block in range(FIRST_BLOCKS)]
+        banks = [(bank(2 * j), bank(2 * j + 1)) for j in range(FIRST_TILES)]
         for g in range(PASSES):
-            for block in range(FIRST_BLOCKS):
-                multiply(banks[block][0], block, g, 0, BIG)
-            for block in range(FIRST_BLOCKS):
-                multiply(banks[block][1], block, g, BIG, E)
-        for block in range(FIRST_BLOCKS):
-            store(*banks[block], block)
+            for j in range(FIRST_TILES):
+                multiply(banks[j][0], j, g, 0, WIDE)
+            for j in range(FIRST_TILES):
+                multiply(banks[j][1], j, g, WIDE, E)
+        for j in range(FIRST_TILES):
+            store(*banks[j], j)
 
         load_piece(2)
 
-        for block in range(FIRST_BLOCKS, last + 1):
-            j = block % FIRST_BLOCKS
-            big, small = bank(2 * j), bank(2 * j + 1)
+        for j in range(FIRST_TILES, last + 1):
+            pair = j % FIRST_TILES
+            wide, narrow = bank(2 * pair), bank(2 * pair + 1)
             for g in range(PASSES):
-                multiply(big, block, g, 0, BIG)
+                multiply(wide, j, g, 0, WIDE)
             for g in range(PASSES):
-                multiply(small, block, g, BIG, E)
-            store(big, small, block)
+                multiply(narrow, j, g, WIDE, E)
+            store(wide, narrow, j)

@@ -124,7 +124,7 @@ def tile_longcatrouter_kernel(tc, x_words, x_scales, w_words, w_scales, out):
         def store(wide, narrow, j):
             logits = results.tile([P, E], F32, name="logits")
             rows = out[P * j : P * (j + 1), :]
-            nc.scalar.copy(out=logits[:, 0:WIDE], in_=wide[:])
+            nc.vector.tensor_copy(out=logits[:, 0:WIDE], in_=wide[:])
             if j < last:
                 nc.vector.tensor_copy(out=logits[:, WIDE:E], in_=narrow[:, 0:NARROW])
                 nc.sync.dma_start(out=rows, in_=logits[:])

@@ -64,7 +64,9 @@ def tile_longcatrouter_kernel(tc, x_words, x_scales, w_words, w_scales, out):
 
         warm = keep.tile([P, NARROW], F32, name="warm")
         zero(warm)
-        for plane in sorted(w_planes + x_planes, key=lambda x: x[1]) + later_planes:
+        x_stage = part("x_stage", *X_SCALE_RUNS[0], 0, FIRST, 1)
+        w_stage = part("w_stage", *W_SCALE_RUNS[0], 0, E, 1)
+        for plane in (x_stage, w_stage, x_planes[0], w_planes[1], x_planes[1]):
             zero(plane[0])
 
         def load_codes(codes, words):
@@ -78,6 +80,14 @@ def tile_longcatrouter_kernel(tc, x_words, x_scales, w_words, w_scales, out):
                 src = scales[g0:g1, r:16:4, c0:c1].rearrange("g q n -> q g n")
                 nc.sync.dma_start(out=tile[r:P:32, :, :].bitcast(I32), in_=src.bitcast(I32))
 
+        def load_quadrant(plane, scales, quadrant):
+            tile, g0, g1, c0, c1 = plane
+            src = scales[g0:g1, 4 * quadrant : 4 * quadrant + 4, c0:c1].rearrange("g r n -> r g n")
+            nc.sync.dma_start(out=tile[32 * quadrant : 32 * quadrant + 4, :, :].bitcast(I32), in_=src.bitcast(I32))
+
+        def move(plane, stage, partitions):
+            nc.vector.tensor_copy(out=plane[0][0:partitions].bitcast(I32), in_=stage[0][0:partitions].bitcast(I32))
+
         def load_piece(i):
             load_codes(later_codes[i][0], x_words)
             load_scales(later_planes[i], x_scales)
@@ -86,8 +96,15 @@ def tile_longcatrouter_kernel(tc, x_words, x_scales, w_words, w_scales, out):
 
         load_codes(x_codes_0[0], x_words)
         load_codes(w_codes_0[0], w_words)
-        load_scales(w_planes[0], w_scales)
-        load_scales(x_planes[0], x_scales)
+        for quadrant in (0, 1):
+            load_quadrant(x_stage, x_scales, quadrant)
+        load_scales(w_stage, w_scales)
+        for quadrant in (2, 3):
+            load_quadrant(x_planes[0], x_scales, quadrant)
+        move(x_planes[0], x_stage, P // 2)
+        move(w_planes[0], w_stage, P)
+        for plane in w_planes[2:] + later_planes:
+            zero(plane[0])
         load_codes(x_codes_0[1], x_words)
         load_codes(w_codes_0[1], w_words)
         for g in range(1, PASSES):

@@ -6,6 +6,7 @@ T, D, E = 4096, 4096, 768
 FLOPS = 2 * T * D * E
 
 F32 = mybir.dt.float32
+BF16 = mybir.dt.bfloat16
 I32 = mybir.dt.int32
 U8 = mybir.dt.uint8
 FP4X4 = mybir.dt.float4_e2m1fn_x4
@@ -20,13 +21,13 @@ WORD = 2
 FIRST_TILES = BANKS // 2
 FIRST = FIRST_TILES * P
 LATER_PIECES = ((FIRST, 2 * FIRST), (2 * FIRST, 4 * FIRST), (4 * FIRST, T))
-START = 2 * P
+START = P
 
 W_SCALE_RUNS = ((0, 2), (2, 5), (5, 8))
 X_SCALE_RUNS = ((0, 3), (3, 8))
-LATER_CODE_RUNS = (((0, PASSES // 2), (PASSES // 2, PASSES)), ((0, PASSES),), ((0, PASSES),))
+LATER_CODE_RUNS = (((0, PASSES // 2), (PASSES // 2, PASSES)), ((0, PASSES // 2), (PASSES // 2, PASSES)), ((0, PASSES),))
 
-WARM_UPS = 3
+WARM_UPS = 5
 RESULT_TILES = 16
 
 
@@ -46,9 +47,8 @@ def tile_longcatrouter_kernel(tc, x_words, x_scales, w_words, w_scales, out):
             tile, g0, g1, first, end = [x for x in parts if x[1] <= g < x[2] and x[3] <= c0 < x[4]][0]
             return tile[:, g - g0, width * (c0 - first) : width * (c1 - first)]
 
-        w_codes_0 = [part("w_codes", 0, 1, e0, e1, WORD) for e0, e1 in ((0, WIDE), (WIDE, E))]
         x_codes_0 = [part("x_codes", 0, 1, t0, t1, WORD) for t0, t1 in ((0, START), (START, FIRST))]
-        w_codes = [part("w_codes", g, g + 1, 0, E, WORD) for g in range(1, PASSES)]
+        w_codes = [part("w_codes", g, g + 1, 0, E, WORD) for g in range(PASSES)]
         x_codes = [part("x_codes", g, g + 1, 0, FIRST, WORD) for g in range(1, PASSES)]
         w_planes = [part("w_planes", g0, g1, 0, E, 1) for g0, g1 in W_SCALE_RUNS]
         x_planes = [part("x_planes", g0, g1, 0, FIRST, 1) for g0, g1 in X_SCALE_RUNS]
@@ -62,11 +62,11 @@ def tile_longcatrouter_kernel(tc, x_words, x_scales, w_words, w_scales, out):
         def zero(tile):
             nc.vector.memset(tile[:].bitcast(I32), 0)
 
-        warm = keep.tile([P, NARROW], F32, name="warm")
+        warm = keep.tile([P, WIDE], BF16, name="warm")
         zero(warm)
         x_stage = part("x_stage", *X_SCALE_RUNS[0], 0, FIRST, 1)
         w_stage = part("w_stage", *W_SCALE_RUNS[0], 0, E, 1)
-        for plane in (x_stage, w_stage, x_planes[0], w_planes[1], x_planes[1]):
+        for plane in (w_stage, x_planes[0], w_planes[1], x_planes[1]):
             zero(plane[0])
 
         def load_codes(codes, words):
@@ -85,8 +85,8 @@ def tile_longcatrouter_kernel(tc, x_words, x_scales, w_words, w_scales, out):
             src = scales[g0:g1, 4 * quadrant : 4 * quadrant + 4, c0:c1].rearrange("g r n -> r g n")
             nc.sync.dma_start(out=tile[32 * quadrant : 32 * quadrant + 4, :, :].bitcast(I32), in_=src.bitcast(I32))
 
-        def move(plane, stage, partitions):
-            nc.vector.tensor_copy(out=plane[0][0:partitions].bitcast(I32), in_=stage[0][0:partitions].bitcast(I32))
+        def move(plane, stage, p0, p1):
+            nc.vector.tensor_copy(out=plane[0][p0:p1].bitcast(I32), in_=stage[0][p0:p1].bitcast(I32))
 
         def load_piece(i):
             load_codes(later_codes[i][0], x_words)
@@ -95,25 +95,25 @@ def tile_longcatrouter_kernel(tc, x_words, x_scales, w_words, w_scales, out):
                 load_codes(codes, x_words)
 
         load_codes(x_codes_0[0], x_words)
-        load_codes(w_codes_0[0], w_words)
         for quadrant in (0, 1):
             load_quadrant(x_stage, x_scales, quadrant)
+        load_codes(w_codes[0], w_words)
         load_scales(w_stage, w_scales)
         for quadrant in (2, 3):
             load_quadrant(x_planes[0], x_scales, quadrant)
-        move(x_planes[0], x_stage, P // 2)
-        move(w_planes[0], w_stage, P)
+        for quadrant in (0, 1):
+            move(x_planes[0], x_stage, 32 * quadrant, 32 * quadrant + 4)
+        move(w_planes[0], w_stage, 0, P)
         for plane in w_planes[2:] + later_planes:
             zero(plane[0])
         load_codes(x_codes_0[1], x_words)
-        load_codes(w_codes_0[1], w_words)
         for g in range(1, PASSES):
             for planes, scales in ((w_planes, w_scales), (x_planes, x_scales)):
                 for plane in planes:
                     if plane[1] == g:
                         load_scales(plane, scales)
             load_codes(x_codes[g - 1], x_words)
-            load_codes(w_codes[g - 1], w_words)
+            load_codes(w_codes[g], w_words)
         load_piece(0)
         load_piece(1)
 
@@ -122,7 +122,7 @@ def tile_longcatrouter_kernel(tc, x_words, x_scales, w_words, w_scales, out):
 
         warm_bank = bank(BANKS - 1)
         for i in range(WARM_UPS):
-            nc.tensor.matmul(warm_bank[:, 0:NARROW], warm[:, 0:P], warm[:], start=True, stop=True)
+            nc.tensor.matmul(warm_bank[:], warm[:, 0:P], warm[:], start=True, stop=True)
 
         def multiply(acc, j, g, e0, e1):
             t0, t1 = P * j, P * (j + 1)
@@ -130,7 +130,7 @@ def tile_longcatrouter_kernel(tc, x_words, x_scales, w_words, w_scales, out):
                 out=acc[:, 0 : e1 - e0],
                 lhsT=operand(all_x_codes, g, t0, t1, WORD).bitcast(FP4X4),
                 lhsT_scale=operand(x_planes + later_planes, g, t0, t1, 1),
-                rhs=operand(w_codes_0 + w_codes, g, e0, e1, WORD).bitcast(FP4X4),
+                rhs=operand(w_codes, g, e0, e1, WORD).bitcast(FP4X4),
                 rhs_scale=operand(w_planes, g, e0, e1, 1),
                 start=(g == 0),
                 stop=(g == PASSES - 1),
@@ -157,7 +157,6 @@ def tile_longcatrouter_kernel(tc, x_words, x_scales, w_words, w_scales, out):
         for g in range(PASSES):
             for j in range(FIRST_TILES):
                 multiply(banks[j][0], j, g, 0, WIDE)
-            for j in range(FIRST_TILES):
                 multiply(banks[j][1], j, g, WIDE, E)
         for j in range(FIRST_TILES):
             store(*banks[j], j)

@@ -21,14 +21,13 @@ WORD = 2
 FIRST_TILES = BANKS // 2
 FIRST = FIRST_TILES * P
 LATER_PIECES = ((FIRST, 2 * FIRST), (2 * FIRST, 4 * FIRST), (4 * FIRST, T))
-START = P
 
 W_SCALE_RUNS = ((0, 2), (2, 5), (5, 8))
 X_SCALE_RUNS = ((0, 3), (3, 8))
-LATER_CODE_RUNS = (((0, PASSES // 2), (PASSES // 2, PASSES)), ((0, PASSES // 2), (PASSES // 2, PASSES)), ((0, PASSES),))
+LATER_CODE_RUNS = (((0, PASSES // 2), (PASSES // 2, PASSES)),) * 3
 
-WARM_UPS = 5
-RESULT_TILES = 16
+WARM_UPS = 6
+RESULT_TILES = 24
 
 
 def tile_longcatrouter_kernel(tc, x_words, x_scales, w_words, w_scales, out):
@@ -47,9 +46,8 @@ def tile_longcatrouter_kernel(tc, x_words, x_scales, w_words, w_scales, out):
             tile, g0, g1, first, end = [x for x in parts if x[1] <= g < x[2] and x[3] <= c0 < x[4]][0]
             return tile[:, g - g0, width * (c0 - first) : width * (c1 - first)]
 
-        x_codes_0 = [part("x_codes", 0, 1, t0, t1, WORD) for t0, t1 in ((0, START), (START, FIRST))]
         w_codes = [part("w_codes", g, g + 1, 0, E, WORD) for g in range(PASSES)]
-        x_codes = [part("x_codes", g, g + 1, 0, FIRST, WORD) for g in range(1, PASSES)]
+        x_codes = [part("x_codes", g, g + 1, 0, FIRST, WORD) for g in range(PASSES)]
         w_planes = [part("w_planes", g0, g1, 0, E, 1) for g0, g1 in W_SCALE_RUNS]
         x_planes = [part("x_planes", g0, g1, 0, FIRST, 1) for g0, g1 in X_SCALE_RUNS]
         later_codes = [
@@ -57,7 +55,7 @@ def tile_longcatrouter_kernel(tc, x_words, x_scales, w_words, w_scales, out):
             for (t0, t1), runs in zip(LATER_PIECES, LATER_CODE_RUNS)
         ]
         later_planes = [part("x_planes", 0, PASSES, t0, t1, 1) for t0, t1 in LATER_PIECES]
-        all_x_codes = x_codes_0 + x_codes + sum(later_codes, [])
+        all_x_codes = x_codes + sum(later_codes, [])
 
         def zero(tile):
             nc.vector.memset(tile[:].bitcast(I32), 0)
@@ -94,9 +92,9 @@ def tile_longcatrouter_kernel(tc, x_words, x_scales, w_words, w_scales, out):
             for codes in later_codes[i][1:]:
                 load_codes(codes, x_words)
 
-        load_codes(x_codes_0[0], x_words)
         for quadrant in (0, 1):
             load_quadrant(x_stage, x_scales, quadrant)
+        load_codes(x_codes[0], x_words)
         load_codes(w_codes[0], w_words)
         load_scales(w_stage, w_scales)
         for quadrant in (2, 3):
@@ -106,14 +104,13 @@ def tile_longcatrouter_kernel(tc, x_words, x_scales, w_words, w_scales, out):
         move(w_planes[0], w_stage, 0, P)
         for plane in w_planes[2:] + later_planes:
             zero(plane[0])
-        load_codes(x_codes_0[1], x_words)
         for g in range(1, PASSES):
             for planes, scales in ((w_planes, w_scales), (x_planes, x_scales)):
                 for plane in planes:
                     if plane[1] == g:
                         load_scales(plane, scales)
-            load_codes(x_codes[g - 1], x_words)
             load_codes(w_codes[g], w_words)
+            load_codes(x_codes[g], x_words)
         load_piece(0)
         load_piece(1)
 
@@ -124,50 +121,75 @@ def tile_longcatrouter_kernel(tc, x_words, x_scales, w_words, w_scales, out):
         for i in range(WARM_UPS):
             nc.tensor.matmul(warm_bank[:], warm[:, 0:P], warm[:], start=True, stop=True)
 
-        def multiply(acc, j, g, e0, e1):
-            t0, t1 = P * j, P * (j + 1)
+        def multiply(acc, stationary, moving, g):
             nc.tensor.matmul_mx(
-                out=acc[:, 0 : e1 - e0],
-                lhsT=operand(all_x_codes, g, t0, t1, WORD).bitcast(FP4X4),
-                lhsT_scale=operand(x_planes + later_planes, g, t0, t1, 1),
-                rhs=operand(w_codes, g, e0, e1, WORD).bitcast(FP4X4),
-                rhs_scale=operand(w_planes, g, e0, e1, 1),
+                out=acc,
+                lhsT=operand(stationary[0], g, stationary[2], stationary[3], WORD).bitcast(FP4X4),
+                lhsT_scale=operand(stationary[1], g, stationary[2], stationary[3], 1),
+                rhs=operand(moving[0], g, moving[2], moving[3], WORD).bitcast(FP4X4),
+                rhs_scale=operand(moving[1], g, moving[2], moving[3], 1),
                 start=(g == 0),
                 stop=(g == PASSES - 1),
             )
 
-        last = T // P - 1
+        def tokens(t0, t1):
+            return all_x_codes, x_planes + later_planes, t0, t1
 
-        def store(wide, narrow, j):
-            logits = results.tile([P, E], F32, name="logits")
-            rows = out[P * j : P * (j + 1), :]
-            nc.vector.tensor_copy(out=logits[:, 0:WIDE], in_=wide[:])
-            if j < last:
-                nc.vector.tensor_copy(out=logits[:, WIDE:E], in_=narrow[:, 0:NARROW])
-                nc.sync.dma_start(out=rows, in_=logits[:])
-            else:
-                nc.sync.dma_start(out=rows[:, 0:WIDE], in_=logits[:, 0:WIDE])
-                half = NARROW // 2
-                for c0 in (0, half):
-                    e0, e1 = WIDE + c0, WIDE + c0 + half
-                    nc.vector.tensor_copy(out=logits[:, e0:e1], in_=narrow[:, c0 : c0 + half])
-                    nc.sync.dma_start(out=rows[:, e0:e1], in_=logits[:, e0:e1])
+        def experts(e0, e1):
+            return w_codes, w_planes, e0, e1
 
-        banks = [(bank(2 * j), bank(2 * j + 1)) for j in range(FIRST_TILES)]
+        def straight(t0):
+            def leave(acc):
+                logits = results.tile([P, WIDE], F32, align_bytes=64, name="logits")
+                nc.vector.tensor_copy(out=logits[:], in_=acc[:])
+                nc.sync.dma_start(out=out[t0 : t0 + P, 0:WIDE], in_=logits[:])
+
+            return tokens(t0, t0 + P), experts(0, WIDE), leave
+
+        def turned(t0, e0):
+            def leave(acc):
+                logits = results.tile([P, WIDE], F32, align_bytes=64, name="logits")
+                nc.vector.transpose(out=logits[:], in_=acc[:])
+                for i in range(4):
+                    rows = out[t0 : t0 + WIDE, e0 + 32 * i : e0 + 32 * (i + 1)].rearrange("(j a) b -> a j b", a=32)
+                    nc.sync.dma_start(out=rows, in_=logits[32 * i : 32 * (i + 1), :].rearrange("a (j b) -> a j b", b=32))
+
+            return experts(e0, e0 + P), tokens(t0, t0 + WIDE), leave
+
+        def chunk(t0):
+            return [straight(t) for t in range(t0, t0 + WIDE, P)] + [turned(t0, e) for e in range(WIDE, E, P)]
+
+        first = chunk(0)
+        banks = [bank(i) for i in range(len(first))]
         for g in range(PASSES):
-            for j in range(FIRST_TILES):
-                multiply(banks[j][0], j, g, 0, WIDE)
-                multiply(banks[j][1], j, g, WIDE, E)
-        for j in range(FIRST_TILES):
-            store(*banks[j], j)
+            for acc, (stationary, moving, leave) in zip(banks, first):
+                multiply(acc[:], stationary, moving, g)
+        for acc, (stationary, moving, leave) in zip(banks, first):
+            leave(acc)
 
         load_piece(2)
 
-        for j in range(FIRST_TILES, last + 1):
-            pair = j % FIRST_TILES
-            wide, narrow = bank(2 * pair), bank(2 * pair + 1)
+        later = sum([chunk(t0) for t0 in range(FIRST, T - WIDE, WIDE)], [])
+        for n, (stationary, moving, leave) in enumerate(later, len(first)):
+            acc = bank(n % BANKS)
             for g in range(PASSES):
-                multiply(wide, j, g, 0, WIDE)
-            for g in range(PASSES):
-                multiply(narrow, j, g, WIDE, E)
-            store(wide, narrow, j)
+                multiply(acc[:], stationary, moving, g)
+            leave(acc)
+
+        for n, t0 in enumerate(range(T - WIDE, T, P)):
+            wide, narrow = [bank((len(first) + len(later) + 2 * n + i) % BANKS) for i in range(2)]
+            for acc, e0, e1 in ((wide, 0, WIDE), (narrow, WIDE, E)):
+                for g in range(PASSES):
+                    multiply(acc[:, 0 : e1 - e0], tokens(t0, t0 + P), experts(e0, e1), g)
+            rows = keep.tile([P, E], F32, name="rows_%d" % n)
+            nc.vector.tensor_copy(out=rows[:, 0:WIDE], in_=wide[:])
+            if t0 < T - P:
+                nc.vector.tensor_copy(out=rows[:, WIDE:E], in_=narrow[:, 0:NARROW])
+                nc.sync.dma_start(out=out[t0 : t0 + P, :], in_=rows[:])
+            else:
+                nc.sync.dma_start(out=out[t0 : t0 + P, 0:WIDE], in_=rows[:, 0:WIDE])
+                half = NARROW // 2
+                for c0 in (0, half):
+                    e0, e1 = WIDE + c0, WIDE + c0 + half
+                    nc.vector.tensor_copy(out=rows[:, e0:e1], in_=narrow[:, c0 : c0 + half])
+                    nc.sync.dma_start(out=out[t0 : t0 + P, e0:e1], in_=rows[:, e0:e1])

@@ -20,13 +20,14 @@ WORD = 2
 
 FIRST_TILES = BANKS // 2
 FIRST = FIRST_TILES * P
+START = 2 * P
 LATER_PIECES = ((FIRST, 2 * FIRST), (2 * FIRST, 4 * FIRST), (4 * FIRST, T))
 
 W_SCALE_RUNS = ((0, 2), (2, 5), (5, 8))
 X_SCALE_RUNS = ((0, 3), (3, 8))
-LATER_CODE_RUNS = (((0, PASSES // 2), (PASSES // 2, PASSES)),) * 3
+LATER_CODE_RUNS = (((0, PASSES // 2), (PASSES // 2, PASSES)), ((0, PASSES),), ((0, PASSES),))
 
-WARM_UPS = 6
+WARM_UPS = 5
 RESULT_TILES = 24
 
 
@@ -67,10 +68,12 @@ def tile_longcatrouter_kernel(tc, x_words, x_scales, w_words, w_scales, out):
         for plane in (w_stage, x_planes[0], w_planes[1], x_planes[1]):
             zero(plane[0])
 
-        def load_codes(codes, words):
-            tile, g0, g1, c0, c1 = codes
+        def load_codes(codes, words, columns=None):
+            tile, g0, g1, first, end = codes
+            c0, c1 = columns or (first, end)
             src = words[g0:g1, :, WORD * c0 : WORD * c1].rearrange("g p n -> p g n")
-            nc.sync.dma_start(out=tile[:].bitcast(I32), in_=src.bitcast(I32))
+            dst = tile[:, :, WORD * (c0 - first) : WORD * (c1 - first)]
+            nc.sync.dma_start(out=dst.bitcast(I32), in_=src.bitcast(I32))
 
         def load_scales(plane, scales):
             tile, g0, g1, c0, c1 = plane
@@ -92,13 +95,15 @@ def tile_longcatrouter_kernel(tc, x_words, x_scales, w_words, w_scales, out):
             for codes in later_codes[i][1:]:
                 load_codes(codes, x_words)
 
+        load_codes(x_codes[0], x_words, (0, START))
+        load_codes(w_codes[0], w_words, (0, WIDE))
         for quadrant in (0, 1):
             load_quadrant(x_stage, x_scales, quadrant)
-        load_codes(x_codes[0], x_words)
-        load_codes(w_codes[0], w_words)
         load_scales(w_stage, w_scales)
         for quadrant in (2, 3):
             load_quadrant(x_planes[0], x_scales, quadrant)
+        load_codes(x_codes[0], x_words, (START, FIRST))
+        load_codes(w_codes[0], w_words, (WIDE, E))
         for quadrant in (0, 1):
             move(x_planes[0], x_stage, 32 * quadrant, 32 * quadrant + 4)
         move(w_planes[0], w_stage, 0, P)

@@ -12,22 +12,24 @@ U8 = mybir.dt.uint8
 FP4X4 = mybir.dt.float4_e2m1fn_x4
 
 P = 128
+QUAD = 32
 PASSES = D // 512
 BANKS = 8
 WIDE = 512
 NARROW = E - WIDE
 WORD = 2
 
-FIRST_TILES = BANKS // 2
-FIRST = FIRST_TILES * P
+TURNED = NARROW // P
+FIRST = (BANKS - TURNED) * P
+LATER_PIECES = ((FIRST, FIRST + WIDE), (FIRST + WIDE, FIRST + 3 * WIDE), (FIRST + 3 * WIDE, T))
+LAST = FIRST + (T - FIRST) // WIDE * WIDE
 START = 2 * P
-LATER_PIECES = ((FIRST, 2 * FIRST), (2 * FIRST, 4 * FIRST), (4 * FIRST, T))
 
 W_SCALE_RUNS = ((0, 2), (2, 5), (5, 8))
 X_SCALE_RUNS = ((0, 3), (3, 8))
 LATER_CODE_RUNS = (((0, PASSES // 2), (PASSES // 2, PASSES)), ((0, PASSES),), ((0, PASSES),))
 
-WARM_UPS = 5
+WARM_UPS = 6
 RESULT_TILES = 24
 
 
@@ -43,7 +45,7 @@ def tile_longcatrouter_kernel(tc, x_words, x_scales, w_words, w_scales, out):
             shape = [P, g1 - g0, width * (c1 - c0)]
             return keep.tile(shape, U8, align_bytes=256, name="%s_%d_%d" % (name, g0, c0)), g0, g1, c0, c1
 
-        def operand(parts, g, c0, c1, width):
+        def window(parts, g, c0, c1, width):
             tile, g0, g1, first, end = [x for x in parts if x[1] <= g < x[2] and x[3] <= c0 < x[4]][0]
             return tile[:, g - g0, width * (c0 - first) : width * (c1 - first)]
 
@@ -56,17 +58,11 @@ def tile_longcatrouter_kernel(tc, x_words, x_scales, w_words, w_scales, out):
             for (t0, t1), runs in zip(LATER_PIECES, LATER_CODE_RUNS)
         ]
         later_planes = [part("x_planes", 0, PASSES, t0, t1, 1) for t0, t1 in LATER_PIECES]
-        all_x_codes = x_codes + sum(later_codes, [])
+        w_stage = part("w_stage", *W_SCALE_RUNS[0], 0, E, 1)
+        x_stage = part("x_stage", *X_SCALE_RUNS[0], 0, FIRST, 1)
 
         def zero(tile):
             nc.vector.memset(tile[:].bitcast(I32), 0)
-
-        warm = keep.tile([P, WIDE], BF16, name="warm")
-        zero(warm)
-        x_stage = part("x_stage", *X_SCALE_RUNS[0], 0, FIRST, 1)
-        w_stage = part("w_stage", *W_SCALE_RUNS[0], 0, E, 1)
-        for plane in (w_stage, x_planes[0], w_planes[1], x_planes[1]):
-            zero(plane[0])
 
         def load_codes(codes, words, columns=None):
             tile, g0, g1, first, end = codes
@@ -79,15 +75,15 @@ def tile_longcatrouter_kernel(tc, x_words, x_scales, w_words, w_scales, out):
             tile, g0, g1, c0, c1 = plane
             for r in range(4):
                 src = scales[g0:g1, r:16:4, c0:c1].rearrange("g q n -> q g n")
-                nc.sync.dma_start(out=tile[r:P:32, :, :].bitcast(I32), in_=src.bitcast(I32))
+                nc.sync.dma_start(out=tile[r:P:QUAD, :, :].bitcast(I32), in_=src.bitcast(I32))
+
+        def live_rows(tile, quadrant):
+            return tile[QUAD * quadrant : QUAD * quadrant + 4].bitcast(I32)
 
         def load_quadrant(plane, scales, quadrant):
             tile, g0, g1, c0, c1 = plane
             src = scales[g0:g1, 4 * quadrant : 4 * quadrant + 4, c0:c1].rearrange("g r n -> r g n")
-            nc.sync.dma_start(out=tile[32 * quadrant : 32 * quadrant + 4, :, :].bitcast(I32), in_=src.bitcast(I32))
-
-        def move(plane, stage, p0, p1):
-            nc.vector.tensor_copy(out=plane[0][p0:p1].bitcast(I32), in_=stage[0][p0:p1].bitcast(I32))
+            nc.sync.dma_start(out=live_rows(tile, quadrant), in_=src.bitcast(I32))
 
         def load_piece(i):
             load_codes(later_codes[i][0], x_words)
@@ -95,18 +91,23 @@ def tile_longcatrouter_kernel(tc, x_words, x_scales, w_words, w_scales, out):
             for codes in later_codes[i][1:]:
                 load_codes(codes, x_words)
 
+        warm = keep.tile([P, WIDE], BF16, name="warm")
+        zero(warm)
+        for plane in (w_stage, x_planes[0], w_planes[1], x_planes[1]):
+            zero(plane[0])
+
         load_codes(x_codes[0], x_words, (0, START))
         load_codes(w_codes[0], w_words, (0, WIDE))
-        for quadrant in (0, 1):
+        for quadrant in (0, 2):
             load_quadrant(x_stage, x_scales, quadrant)
         load_scales(w_stage, w_scales)
-        for quadrant in (2, 3):
+        for quadrant in (1, 3):
             load_quadrant(x_planes[0], x_scales, quadrant)
         load_codes(x_codes[0], x_words, (START, FIRST))
         load_codes(w_codes[0], w_words, (WIDE, E))
-        for quadrant in (0, 1):
-            move(x_planes[0], x_stage, 32 * quadrant, 32 * quadrant + 4)
-        move(w_planes[0], w_stage, 0, P)
+        for quadrant in (0, 2):
+            nc.vector.tensor_copy(out=live_rows(x_planes[0][0], quadrant), in_=live_rows(x_stage[0], quadrant))
+        nc.vector.tensor_copy(out=w_planes[0][0][:].bitcast(I32), in_=w_stage[0][:].bitcast(I32))
         for plane in w_planes[2:] + later_planes:
             zero(plane[0])
         for g in range(1, PASSES):
@@ -120,28 +121,28 @@ def tile_longcatrouter_kernel(tc, x_words, x_scales, w_words, w_scales, out):
         load_piece(1)
 
         def bank(i):
-            return psum.tile([P, WIDE], F32, tag="bank%d" % i, name="bank%d" % i)
+            return psum.tile([P, WIDE], F32, tag="bank%d" % (i % BANKS), name="bank%d" % (i % BANKS))
 
         warm_bank = bank(BANKS - 1)
         for i in range(WARM_UPS):
             nc.tensor.matmul(warm_bank[:], warm[:, 0:P], warm[:], start=True, stop=True)
 
-        def multiply(acc, stationary, moving, g):
-            nc.tensor.matmul_mx(
-                out=acc,
-                lhsT=operand(stationary[0], g, stationary[2], stationary[3], WORD).bitcast(FP4X4),
-                lhsT_scale=operand(stationary[1], g, stationary[2], stationary[3], 1),
-                rhs=operand(moving[0], g, moving[2], moving[3], WORD).bitcast(FP4X4),
-                rhs_scale=operand(moving[1], g, moving[2], moving[3], 1),
-                start=(g == 0),
-                stop=(g == PASSES - 1),
-            )
-
         def tokens(t0, t1):
-            return all_x_codes, x_planes + later_planes, t0, t1
+            return x_codes + sum(later_codes, []), x_planes + later_planes, t0, t1
 
         def experts(e0, e1):
             return w_codes, w_planes, e0, e1
+
+        def multiply(acc, stationary, moving, g):
+            nc.tensor.matmul_mx(
+                out=acc[:, 0 : moving[3] - moving[2]],
+                lhsT=window(stationary[0], g, *stationary[2:], WORD).bitcast(FP4X4),
+                lhsT_scale=window(stationary[1], g, *stationary[2:], 1),
+                rhs=window(moving[0], g, *moving[2:], WORD).bitcast(FP4X4),
+                rhs_scale=window(moving[1], g, *moving[2:], 1),
+                start=(g == 0),
+                stop=(g == PASSES - 1),
+            )
 
         def straight(t0):
             def leave(acc):
@@ -155,46 +156,55 @@ def tile_longcatrouter_kernel(tc, x_words, x_scales, w_words, w_scales, out):
             def leave(acc):
                 logits = results.tile([P, WIDE], F32, align_bytes=64, name="logits")
                 nc.vector.transpose(out=logits[:], in_=acc[:])
-                for i in range(4):
-                    rows = out[t0 : t0 + WIDE, e0 + 32 * i : e0 + 32 * (i + 1)].rearrange("(j a) b -> a j b", a=32)
-                    nc.sync.dma_start(out=rows, in_=logits[32 * i : 32 * (i + 1), :].rearrange("a (j b) -> a j b", b=32))
+                for i in range(P // QUAD):
+                    dst = out[t0 : t0 + WIDE, e0 + QUAD * i : e0 + QUAD * (i + 1)].rearrange("(j a) b -> a j b", a=QUAD)
+                    src = logits[QUAD * i : QUAD * (i + 1), :].rearrange("a (j b) -> a j b", b=QUAD)
+                    nc.sync.dma_start(out=dst, in_=src)
 
             return experts(e0, e0 + P), tokens(t0, t0 + WIDE), leave
 
-        def chunk(t0):
-            return [straight(t) for t in range(t0, t0 + WIDE, P)] + [turned(t0, e) for e in range(WIDE, E, P)]
+        def whole_rows(t0):
+            rows = keep.tile([P, E], F32, name="rows_%d" % t0)
 
-        first = chunk(0)
-        banks = [bank(i) for i in range(len(first))]
+            def leave_wide(acc):
+                nc.vector.tensor_copy(out=rows[:, 0:WIDE], in_=acc[:])
+                if t0 == T - P:
+                    nc.sync.dma_start(out=out[t0:T, 0:WIDE], in_=rows[:, 0:WIDE])
+
+            def leave_narrow(acc):
+                if t0 < T - P:
+                    nc.vector.tensor_copy(out=rows[:, WIDE:E], in_=acc[:, 0:NARROW])
+                    nc.sync.dma_start(out=out[t0 : t0 + P, :], in_=rows[:])
+                else:
+                    for c0 in (0, NARROW // 2):
+                        e0, e1 = WIDE + c0, WIDE + c0 + NARROW // 2
+                        nc.vector.tensor_copy(out=rows[:, e0:e1], in_=acc[:, c0 : c0 + NARROW // 2])
+                        nc.sync.dma_start(out=out[t0:T, e0:e1], in_=rows[:, e0:e1])
+
+            return (tokens(t0, t0 + P), experts(0, WIDE), leave_wide), (tokens(t0, t0 + P), experts(WIDE, E), leave_narrow)
+
+        def chunk(t0):
+            return [straight(t) for t in range(t0, t0 + WIDE, P)], [turned(t0, e0) for e0 in range(WIDE, E, P)]
+
+        first_straight, first_turned = chunk(0)
+        extra = [whole_rows(t0) for t0 in range(WIDE, FIRST, P)]
+        first = first_straight + [wide for wide, narrow in extra] + first_turned
+        banks = [bank(i) for i in range(BANKS)]
         for g in range(PASSES):
             for acc, (stationary, moving, leave) in zip(banks, first):
-                multiply(acc[:], stationary, moving, g)
+                multiply(acc, stationary, moving, g)
         for acc, (stationary, moving, leave) in zip(banks, first):
             leave(acc)
 
         load_piece(2)
 
-        later = sum([chunk(t0) for t0 in range(FIRST, T - WIDE, WIDE)], [])
-        for n, (stationary, moving, leave) in enumerate(later, len(first)):
-            acc = bank(n % BANKS)
+        later = [narrow for wide, narrow in extra]
+        for t0 in range(FIRST, LAST, WIDE):
+            later += sum(chunk(t0), [])
+        for t0 in range(LAST, T, P):
+            later += whole_rows(t0)
+        for i, (stationary, moving, leave) in enumerate(later):
+            acc = bank(i)
             for g in range(PASSES):
-                multiply(acc[:], stationary, moving, g)
+                multiply(acc, stationary, moving, g)
             leave(acc)
-
-        for n, t0 in enumerate(range(T - WIDE, T, P)):
-            wide, narrow = [bank((len(first) + len(later) + 2 * n + i) % BANKS) for i in range(2)]
-            for acc, e0, e1 in ((wide, 0, WIDE), (narrow, WIDE, E)):
-                for g in range(PASSES):
-                    multiply(acc[:, 0 : e1 - e0], tokens(t0, t0 + P), experts(e0, e1), g)
-            rows = keep.tile([P, E], F32, name="rows_%d" % n)
-            nc.vector.tensor_copy(out=rows[:, 0:WIDE], in_=wide[:])
-            if t0 < T - P:
-                nc.vector.tensor_copy(out=rows[:, WIDE:E], in_=narrow[:, 0:NARROW])
-                nc.sync.dma_start(out=out[t0 : t0 + P, :], in_=rows[:])
-            else:
-                nc.sync.dma_start(out=out[t0 : t0 + P, 0:WIDE], in_=rows[:, 0:WIDE])
-                half = NARROW // 2
-                for c0 in (0, half):
-                    e0, e1 = WIDE + c0, WIDE + c0 + half
-                    nc.vector.tensor_copy(out=rows[:, e0:e1], in_=narrow[:, c0 : c0 + half])
-                    nc.sync.dma_start(out=out[t0 : t0 + P, e0:e1], in_=rows[:, e0:e1])

@@ -19,25 +19,22 @@ WIDE = 512
 NARROW = E - WIDE
 WORD = 2
 
-TURNED = NARROW // P
-FIRST = (BANKS - TURNED) * P
-LATER_PIECES = ((FIRST, FIRST + WIDE), (FIRST + WIDE, FIRST + 3 * WIDE), (FIRST + 3 * WIDE, T))
-LAST = FIRST + (T - FIRST) // WIDE * WIDE
+FIRST = BANKS // 2 * P
+LATER_PIECES = ((FIRST, 2 * FIRST), (2 * FIRST, 4 * FIRST), (4 * FIRST, T))
+LAST = T - WIDE
 START = 2 * P
 
 W_SCALE_RUNS = ((0, 2), (2, 5), (5, 8))
 X_SCALE_RUNS = ((0, 3), (3, 8))
 LATER_CODE_RUNS = (((0, PASSES // 2), (PASSES // 2, PASSES)), ((0, PASSES),), ((0, PASSES),))
 
-WARM_UPS = 6
-RESULT_TILES = 24
+WARM_UPS = 5
 
 
 def tile_longcatrouter_kernel(tc, x_words, x_scales, w_words, w_scales, out):
     nc = tc.nc
     with ExitStack() as ctx:
         keep = ctx.enter_context(tc.tile_pool(name="keep", bufs=1))
-        results = ctx.enter_context(tc.tile_pool(name="results", bufs=RESULT_TILES))
         psum = ctx.enter_context(tc.psum_pool(name="psum", bufs=1))
         ctx.enter_context(tc.manual_schedule())
 
@@ -92,21 +89,18 @@ def tile_longcatrouter_kernel(tc, x_words, x_scales, w_words, w_scales, out):
                 load_codes(codes, x_words)
 
         warm = keep.tile([P, WIDE], BF16, name="warm")
-        zero(warm)
-        for plane in (w_stage, x_planes[0], w_planes[1], x_planes[1]):
-            zero(plane[0])
+        for tile in (warm, w_stage[0], x_planes[0][0], w_planes[1][0], x_planes[1][0]):
+            zero(tile)
 
         load_codes(x_codes[0], x_words, (0, START))
-        load_codes(w_codes[0], w_words, (0, WIDE))
-        for quadrant in (0, 2):
-            load_quadrant(x_stage, x_scales, quadrant)
-        load_scales(w_stage, w_scales)
-        for quadrant in (1, 3):
-            load_quadrant(x_planes[0], x_scales, quadrant)
-        load_codes(x_codes[0], x_words, (START, FIRST))
         load_codes(w_codes[0], w_words, (WIDE, E))
-        for quadrant in (0, 2):
-            nc.vector.tensor_copy(out=live_rows(x_planes[0][0], quadrant), in_=live_rows(x_stage[0], quadrant))
+        load_quadrant(x_stage, x_scales, 0)
+        load_scales(w_stage, w_scales)
+        for quadrant in (2, 1, 3):
+            load_quadrant(x_planes[0], x_scales, quadrant)
+        load_codes(w_codes[0], w_words, (0, WIDE))
+        load_codes(x_codes[0], x_words, (START, FIRST))
+        nc.vector.tensor_copy(out=live_rows(x_planes[0][0], 0), in_=live_rows(x_stage[0], 0))
         nc.vector.tensor_copy(out=w_planes[0][0][:].bitcast(I32), in_=w_stage[0][:].bitcast(I32))
         for plane in w_planes[2:] + later_planes:
             zero(plane[0])
@@ -144,17 +138,17 @@ def tile_longcatrouter_kernel(tc, x_words, x_scales, w_words, w_scales, out):
                 stop=(g == PASSES - 1),
             )
 
-        def straight(t0):
+        def straight(t0, e0, e1):
             def leave(acc):
-                logits = results.tile([P, WIDE], F32, align_bytes=64, name="logits")
-                nc.vector.tensor_copy(out=logits[:], in_=acc[:])
-                nc.sync.dma_start(out=out[t0 : t0 + P, 0:WIDE], in_=logits[:])
+                logits = keep.tile([P, e1 - e0], F32, name="straight_%d_%d" % (t0, e0))
+                nc.vector.tensor_copy(out=logits[:], in_=acc[:, 0 : e1 - e0])
+                nc.sync.dma_start(out=out[t0 : t0 + P, e0:e1], in_=logits[:])
 
-            return tokens(t0, t0 + P), experts(0, WIDE), leave
+            return tokens(t0, t0 + P), experts(e0, e1), leave
 
         def turned(t0, e0):
             def leave(acc):
-                logits = results.tile([P, WIDE], F32, align_bytes=64, name="logits")
+                logits = keep.tile([P, WIDE], F32, align_bytes=64, name="turned_%d_%d" % (t0, e0))
                 nc.vector.transpose(out=logits[:], in_=acc[:])
                 for i in range(P // QUAD):
                     dst = out[t0 : t0 + WIDE, e0 + QUAD * i : e0 + QUAD * (i + 1)].rearrange("(j a) b -> a j b", a=QUAD)
@@ -163,32 +157,26 @@ def tile_longcatrouter_kernel(tc, x_words, x_scales, w_words, w_scales, out):
 
             return experts(e0, e0 + P), tokens(t0, t0 + WIDE), leave
 
-        def whole_rows(t0):
+        def whole_rows(t0, narrow_first):
             rows = keep.tile([P, E], F32, name="rows_%d" % t0)
 
-            def leave_wide(acc):
-                nc.vector.tensor_copy(out=rows[:, 0:WIDE], in_=acc[:])
-                if t0 == T - P:
-                    nc.sync.dma_start(out=out[t0:T, 0:WIDE], in_=rows[:, 0:WIDE])
+            def group(e0, e1, completes):
+                def leave(acc):
+                    nc.vector.tensor_copy(out=rows[:, e0:e1], in_=acc[:, 0 : e1 - e0])
+                    if completes:
+                        nc.sync.dma_start(out=out[t0 : t0 + P, :], in_=rows[:])
 
-            def leave_narrow(acc):
-                if t0 < T - P:
-                    nc.vector.tensor_copy(out=rows[:, WIDE:E], in_=acc[:, 0:NARROW])
-                    nc.sync.dma_start(out=out[t0 : t0 + P, :], in_=rows[:])
-                else:
-                    for c0 in (0, NARROW // 2):
-                        e0, e1 = WIDE + c0, WIDE + c0 + NARROW // 2
-                        nc.vector.tensor_copy(out=rows[:, e0:e1], in_=acc[:, c0 : c0 + NARROW // 2])
-                        nc.sync.dma_start(out=out[t0:T, e0:e1], in_=rows[:, e0:e1])
+                return tokens(t0, t0 + P), experts(e0, e1), leave
 
-            return (tokens(t0, t0 + P), experts(0, WIDE), leave_wide), (tokens(t0, t0 + P), experts(WIDE, E), leave_narrow)
+            return [group(0, WIDE, narrow_first), group(WIDE, E, not narrow_first)]
 
         def chunk(t0):
-            return [straight(t) for t in range(t0, t0 + WIDE, P)], [turned(t0, e0) for e0 in range(WIDE, E, P)]
+            return [straight(t, 0, WIDE) for t in range(t0, t0 + WIDE, P)] + [turned(t0, e0) for e0 in range(WIDE, E, P)]
 
-        first_straight, first_turned = chunk(0)
-        extra = [whole_rows(t0) for t0 in range(WIDE, FIRST, P)]
-        first = first_straight + [wide for wide, narrow in extra] + first_turned
+        first = []
+        for t0 in range(0, FIRST, START):
+            pairs = [whole_rows(t, True) for t in range(t0, t0 + START, P)]
+            first += [narrow for wide, narrow in pairs] + [wide for wide, narrow in pairs]
         banks = [bank(i) for i in range(BANKS)]
         for g in range(PASSES):
             for acc, (stationary, moving, leave) in zip(banks, first):
@@ -198,11 +186,12 @@ def tile_longcatrouter_kernel(tc, x_words, x_scales, w_words, w_scales, out):
 
         load_piece(2)
 
-        later = [narrow for wide, narrow in extra]
+        later = []
         for t0 in range(FIRST, LAST, WIDE):
-            later += sum(chunk(t0), [])
-        for t0 in range(LAST, T, P):
-            later += whole_rows(t0)
+            later += chunk(t0)
+        for t0 in range(LAST, T - P, P):
+            later += whole_rows(t0, False)
+        later += [straight(T - P, 0, WIDE)] + [straight(T - P, e0, e0 + P) for e0 in range(WIDE, E, P)]
         for i, (stationary, moving, leave) in enumerate(later):
             acc = bank(i)
             for g in range(PASSES):

@@ -28,7 +28,7 @@ W_SCALE_RUNS = ((0, 2), (2, 5), (5, 8))
 X_SCALE_RUNS = ((0, 3), (3, 8))
 LATER_CODE_RUNS = (((0, PASSES // 2), (PASSES // 2, PASSES)), ((0, PASSES),), ((0, PASSES),))
 
-WARM_UPS = 5
+WARM_UPS = 6
 
 
 def tile_longcatrouter_kernel(tc, x_words, x_scales, w_words, w_scales, out):

@@ -19,16 +19,15 @@ WIDE = 512
 NARROW = E - WIDE
 WORD = 2
 
-FIRST = BANKS // 2 * P
+FIRST = WIDE
 LATER_PIECES = ((FIRST, 2 * FIRST), (2 * FIRST, 4 * FIRST), (4 * FIRST, T))
 LAST = T - WIDE
-START = 2 * P
 
 W_SCALE_RUNS = ((0, 2), (2, 5), (5, 8))
 X_SCALE_RUNS = ((0, 3), (3, 8))
-LATER_CODE_RUNS = (((0, PASSES // 2), (PASSES // 2, PASSES)), ((0, PASSES),), ((0, PASSES),))
+LATER_CODE_RUNS = (((0, PASSES // 2), (PASSES // 2, PASSES)),) * 3
 
-WARM_UPS = 6
+WARM_UPS = 5
 
 
 def tile_longcatrouter_kernel(tc, x_words, x_scales, w_words, w_scales, out):
@@ -61,26 +60,24 @@ def tile_longcatrouter_kernel(tc, x_words, x_scales, w_words, w_scales, out):
         def zero(tile):
             nc.vector.memset(tile[:].bitcast(I32), 0)
 
-        def load_codes(codes, words, columns=None):
-            tile, g0, g1, first, end = codes
-            c0, c1 = columns or (first, end)
+        def load_codes(codes, words, queue=nc.sync):
+            tile, g0, g1, c0, c1 = codes
             src = words[g0:g1, :, WORD * c0 : WORD * c1].rearrange("g p n -> p g n")
-            dst = tile[:, :, WORD * (c0 - first) : WORD * (c1 - first)]
-            nc.sync.dma_start(out=dst.bitcast(I32), in_=src.bitcast(I32))
+            queue.dma_start(out=tile[:].bitcast(I32), in_=src.bitcast(I32))
 
-        def load_scales(plane, scales):
+        def load_scales(plane, scales, queues=(nc.sync,)):
             tile, g0, g1, c0, c1 = plane
             for r in range(4):
                 src = scales[g0:g1, r:16:4, c0:c1].rearrange("g q n -> q g n")
-                nc.sync.dma_start(out=tile[r:P:QUAD, :, :].bitcast(I32), in_=src.bitcast(I32))
+                queues[r % len(queues)].dma_start(out=tile[r:P:QUAD, :, :].bitcast(I32), in_=src.bitcast(I32))
 
         def live_rows(tile, quadrant):
             return tile[QUAD * quadrant : QUAD * quadrant + 4].bitcast(I32)
 
-        def load_quadrant(plane, scales, quadrant):
+        def load_quadrant(plane, scales, quadrant, queue):
             tile, g0, g1, c0, c1 = plane
             src = scales[g0:g1, 4 * quadrant : 4 * quadrant + 4, c0:c1].rearrange("g r n -> r g n")
-            nc.sync.dma_start(out=live_rows(tile, quadrant), in_=src.bitcast(I32))
+            queue.dma_start(out=live_rows(tile, quadrant), in_=src.bitcast(I32))
 
         def load_piece(i):
             load_codes(later_codes[i][0], x_words)
@@ -89,20 +86,20 @@ def tile_longcatrouter_kernel(tc, x_words, x_scales, w_words, w_scales, out):
                 load_codes(codes, x_words)
 
         warm = keep.tile([P, WIDE], BF16, name="warm")
-        for tile in (warm, w_stage[0], x_planes[0][0], w_planes[1][0], x_planes[1][0]):
+        for tile in (warm, w_stage[0], x_planes[0][0], w_planes[1][0]):
             zero(tile)
 
-        load_codes(x_codes[0], x_words, (0, START))
-        load_codes(w_codes[0], w_words, (WIDE, E))
-        load_quadrant(x_stage, x_scales, 0)
-        load_scales(w_stage, w_scales)
-        for quadrant in (2, 1, 3):
-            load_quadrant(x_planes[0], x_scales, quadrant)
-        load_codes(w_codes[0], w_words, (0, WIDE))
-        load_codes(x_codes[0], x_words, (START, FIRST))
-        nc.vector.tensor_copy(out=live_rows(x_planes[0][0], 0), in_=live_rows(x_stage[0], 0))
+        load_quadrant(x_stage, x_scales, 0, nc.sync)
+        load_quadrant(x_stage, x_scales, 2, nc.scalar)
+        load_codes(w_codes[0], w_words, nc.sync)
+        load_codes(x_codes[0], x_words, nc.scalar)
+        load_scales(w_stage, w_scales, (nc.sync, nc.scalar))
+        load_quadrant(x_planes[0], x_scales, 1, nc.sync)
+        load_quadrant(x_planes[0], x_scales, 3, nc.scalar)
+        for quadrant in (0, 2):
+            nc.vector.tensor_copy(out=live_rows(x_planes[0][0], quadrant), in_=live_rows(x_stage[0], quadrant))
         nc.vector.tensor_copy(out=w_planes[0][0][:].bitcast(I32), in_=w_stage[0][:].bitcast(I32))
-        for plane in w_planes[2:] + later_planes:
+        for plane in x_planes[1:] + w_planes[2:] + later_planes:
             zero(plane[0])
         for g in range(1, PASSES):
             for planes, scales in ((w_planes, w_scales), (x_planes, x_scales)):
@@ -157,7 +154,7 @@ def tile_longcatrouter_kernel(tc, x_words, x_scales, w_words, w_scales, out):
 
             return experts(e0, e0 + P), tokens(t0, t0 + WIDE), leave
 
-        def whole_rows(t0, narrow_first):
+        def whole_rows(t0):
             rows = keep.tile([P, E], F32, name="rows_%d" % t0)
 
             def group(e0, e1, completes):
@@ -168,16 +165,13 @@ def tile_longcatrouter_kernel(tc, x_words, x_scales, w_words, w_scales, out):
 
                 return tokens(t0, t0 + P), experts(e0, e1), leave
 
-            return [group(0, WIDE, narrow_first), group(WIDE, E, not narrow_first)]
+            return [group(0, WIDE, False), group(WIDE, E, True)]
 
         def chunk(t0):
             return [straight(t, 0, WIDE) for t in range(t0, t0 + WIDE, P)] + [turned(t0, e0) for e0 in range(WIDE, E, P)]
 
-        first = []
-        for t0 in range(0, FIRST, START):
-            pairs = [whole_rows(t, True) for t in range(t0, t0 + START, P)]
-            first += [narrow for wide, narrow in pairs] + [wide for wide, narrow in pairs]
-        banks = [bank(i) for i in range(BANKS)]
+        first = chunk(0)
+        banks = [bank(i) for i in range(len(first))]
         for g in range(PASSES):
             for acc, (stationary, moving, leave) in zip(banks, first):
                 multiply(acc, stationary, moving, g)
@@ -190,10 +184,10 @@ def tile_longcatrouter_kernel(tc, x_words, x_scales, w_words, w_scales, out):
         for t0 in range(FIRST, LAST, WIDE):
             later += chunk(t0)
         for t0 in range(LAST, T - P, P):
-            later += whole_rows(t0, False)
+            later += whole_rows(t0)
         later += [straight(T - P, 0, WIDE)] + [straight(T - P, e0, e0 + P) for e0 in range(WIDE, E, P)]
         for i, (stationary, moving, leave) in enumerate(later):
-            acc = bank(i)
+            acc = bank(len(first) + i)
             for g in range(PASSES):
                 multiply(acc, stationary, moving, g)
             leave(acc)

@@ -16,18 +16,20 @@ QUAD = 32
 PASSES = D // 512
 BANKS = 8
 WIDE = 512
-NARROW = E - WIDE
 WORD = 2
+TURNED = range(WIDE, E, P)
 
-FIRST = WIDE
-LATER_PIECES = ((FIRST, 2 * FIRST), (2 * FIRST, 4 * FIRST), (4 * FIRST, T))
-LAST = T - WIDE
+FIRST = (BANKS - len(TURNED)) * P
+LATER_PIECES = ((FIRST, FIRST + WIDE), (FIRST + WIDE, FIRST + 3 * WIDE), (FIRST + 3 * WIDE, T))
+LAST = T - (T - FIRST) % WIDE
+START = WIDE // 2
 
-W_SCALE_RUNS = ((0, 2), (2, 5), (5, 8))
-X_SCALE_RUNS = ((0, 3), (3, 8))
-LATER_CODE_RUNS = (((0, PASSES // 2), (PASSES // 2, PASSES)),) * 3
+W_SCALE_RUNS = ((0, 2), (2, 4), (4, 8))
+X_SCALE_RUNS = ((0, 1), (1, 3), (3, 8))
+HALVES = ((0, PASSES // 2), (PASSES // 2, PASSES))
+LATER_CODE_RUNS = (HALVES, ((0, PASSES),), HALVES)
 
-WARM_UPS = 5
+WARM_UPS = 6
 
 
 def tile_longcatrouter_kernel(tc, x_words, x_scales, w_words, w_scales, out):
@@ -60,24 +62,26 @@ def tile_longcatrouter_kernel(tc, x_words, x_scales, w_words, w_scales, out):
         def zero(tile):
             nc.vector.memset(tile[:].bitcast(I32), 0)
 
-        def load_codes(codes, words, queue=nc.sync):
-            tile, g0, g1, c0, c1 = codes
+        def load_codes(codes, words, columns=None):
+            tile, g0, g1, first, end = codes
+            c0, c1 = columns or (first, end)
             src = words[g0:g1, :, WORD * c0 : WORD * c1].rearrange("g p n -> p g n")
-            queue.dma_start(out=tile[:].bitcast(I32), in_=src.bitcast(I32))
+            dst = tile[:, :, WORD * (c0 - first) : WORD * (c1 - first)]
+            nc.sync.dma_start(out=dst.bitcast(I32), in_=src.bitcast(I32))
 
-        def load_scales(plane, scales, queues=(nc.sync,)):
+        def load_scales(plane, scales):
             tile, g0, g1, c0, c1 = plane
             for r in range(4):
                 src = scales[g0:g1, r:16:4, c0:c1].rearrange("g q n -> q g n")
-                queues[r % len(queues)].dma_start(out=tile[r:P:QUAD, :, :].bitcast(I32), in_=src.bitcast(I32))
+                nc.sync.dma_start(out=tile[r:P:QUAD, :, :].bitcast(I32), in_=src.bitcast(I32))
 
         def live_rows(tile, quadrant):
             return tile[QUAD * quadrant : QUAD * quadrant + 4].bitcast(I32)
 
-        def load_quadrant(plane, scales, quadrant, queue):
+        def load_quadrant(plane, scales, quadrant):
             tile, g0, g1, c0, c1 = plane
             src = scales[g0:g1, 4 * quadrant : 4 * quadrant + 4, c0:c1].rearrange("g r n -> r g n")
-            queue.dma_start(out=live_rows(tile, quadrant), in_=src.bitcast(I32))
+            nc.sync.dma_start(out=live_rows(tile, quadrant), in_=src.bitcast(I32))
 
         def load_piece(i):
             load_codes(later_codes[i][0], x_words)
@@ -85,29 +89,29 @@ def tile_longcatrouter_kernel(tc, x_words, x_scales, w_words, w_scales, out):
             for codes in later_codes[i][1:]:
                 load_codes(codes, x_words)
 
-        warm = keep.tile([P, WIDE], BF16, name="warm")
-        for tile in (warm, w_stage[0], x_planes[0][0], w_planes[1][0]):
+        warm = keep.tile([P, P], BF16, name="warm")
+        for tile in (warm, w_stage[0], x_planes[0][0], x_planes[1][0]):
             zero(tile)
 
-        load_quadrant(x_stage, x_scales, 0, nc.sync)
-        load_quadrant(x_stage, x_scales, 2, nc.scalar)
-        load_codes(w_codes[0], w_words, nc.sync)
-        load_codes(x_codes[0], x_words, nc.scalar)
-        load_scales(w_stage, w_scales, (nc.sync, nc.scalar))
-        load_quadrant(x_planes[0], x_scales, 1, nc.sync)
-        load_quadrant(x_planes[0], x_scales, 3, nc.scalar)
-        for quadrant in (0, 2):
-            nc.vector.tensor_copy(out=live_rows(x_planes[0][0], quadrant), in_=live_rows(x_stage[0], quadrant))
+        load_codes(x_codes[0], x_words, (0, START))
+        load_codes(w_codes[0], w_words, (WIDE, E))
+        load_quadrant(x_stage, x_scales, 0)
+        load_scales(w_stage, w_scales)
+        for quadrant in (2, 1, 3):
+            load_quadrant(x_planes[0], x_scales, quadrant)
+        load_codes(w_codes[0], w_words, (0, WIDE))
+        load_codes(x_codes[0], x_words, (START, FIRST))
+        nc.vector.tensor_copy(out=live_rows(x_planes[0][0], 0), in_=live_rows(x_stage[0], 0))
         nc.vector.tensor_copy(out=w_planes[0][0][:].bitcast(I32), in_=w_stage[0][:].bitcast(I32))
-        for plane in x_planes[1:] + w_planes[2:] + later_planes:
+        for plane in [w_planes[1], x_planes[2], w_planes[2]] + later_planes:
             zero(plane[0])
         for g in range(1, PASSES):
+            load_codes(w_codes[g], w_words)
+            load_codes(x_codes[g], x_words)
             for planes, scales in ((w_planes, w_scales), (x_planes, x_scales)):
                 for plane in planes:
                     if plane[1] == g:
                         load_scales(plane, scales)
-            load_codes(w_codes[g], w_words)
-            load_codes(x_codes[g], x_words)
         load_piece(0)
         load_piece(1)
 
@@ -115,8 +119,9 @@ def tile_longcatrouter_kernel(tc, x_words, x_scales, w_words, w_scales, out):
             return psum.tile([P, WIDE], F32, tag="bank%d" % (i % BANKS), name="bank%d" % (i % BANKS))
 
         warm_bank = bank(BANKS - 1)
+        warm_columns = warm[:].unsqueeze(1).to_broadcast([P, WIDE // P, P])
         for i in range(WARM_UPS):
-            nc.tensor.matmul(warm_bank[:], warm[:, 0:P], warm[:], start=True, stop=True)
+            nc.tensor.matmul(warm_bank[:], warm[:], warm_columns, start=True, stop=True)
 
         def tokens(t0, t1):
             return x_codes + sum(later_codes, []), x_planes + later_planes, t0, t1
@@ -124,14 +129,15 @@ def tile_longcatrouter_kernel(tc, x_words, x_scales, w_words, w_scales, out):
         def experts(e0, e1):
             return w_codes, w_planes, e0, e1
 
-        def multiply(acc, stationary, moving, g):
+        def multiply(acc, stationary, moving, g, columns=None):
+            c0, c1 = columns or moving[2:]
             nc.tensor.matmul_mx(
-                out=acc[:, 0 : moving[3] - moving[2]],
+                out=acc[:, c0 - moving[2] : c1 - moving[2]],
                 lhsT=window(stationary[0], g, *stationary[2:], WORD).bitcast(FP4X4),
                 lhsT_scale=window(stationary[1], g, *stationary[2:], 1),
-                rhs=window(moving[0], g, *moving[2:], WORD).bitcast(FP4X4),
-                rhs_scale=window(moving[1], g, *moving[2:], 1),
-                start=(g == 0),
+                rhs=window(moving[0], g, c0, c1, WORD).bitcast(FP4X4),
+                rhs_scale=window(moving[1], g, c0, c1, 1),
+                start=(g == 0 and c0 == moving[2]),
                 stop=(g == PASSES - 1),
             )
 
@@ -157,37 +163,59 @@ def tile_longcatrouter_kernel(tc, x_words, x_scales, w_words, w_scales, out):
         def whole_rows(t0):
             rows = keep.tile([P, E], F32, name="rows_%d" % t0)
 
-            def group(e0, e1, completes):
+            def group(e0, e1):
                 def leave(acc):
                     nc.vector.tensor_copy(out=rows[:, e0:e1], in_=acc[:, 0 : e1 - e0])
-                    if completes:
+                    if e1 == E:
                         nc.sync.dma_start(out=out[t0 : t0 + P, :], in_=rows[:])
 
                 return tokens(t0, t0 + P), experts(e0, e1), leave
 
-            return [group(0, WIDE, False), group(WIDE, E, True)]
+            return [group(0, WIDE), group(WIDE, E)]
 
-        def chunk(t0):
-            return [straight(t, 0, WIDE) for t in range(t0, t0 + WIDE, P)] + [turned(t0, e0) for e0 in range(WIDE, E, P)]
+        def four_straight(t0):
+            rows = keep.tile([P, WIDE // P, WIDE], F32, name="four_%d" % t0)
 
-        first = chunk(0)
-        banks = [bank(i) for i in range(len(first))]
-        for g in range(PASSES):
-            for acc, (stationary, moving, leave) in zip(banks, first):
+            def group(i):
+                def leave(acc):
+                    nc.vector.tensor_copy(out=rows[:, i, :], in_=acc[:])
+                    if i == WIDE // P - 1:
+                        dst = out[t0 : t0 + WIDE, 0:WIDE].rearrange("(i p) e -> p i e", p=P)
+                        nc.sync.dma_start(out=dst, in_=rows[:])
+
+                return tokens(t0 + P * i, t0 + P * (i + 1)), experts(0, WIDE), leave
+
+            return [group(i) for i in range(WIDE // P)]
+
+        beyond = [whole_rows(t0) for t0 in range(WIDE, FIRST, P)]
+        first = [turned(0, e0) for e0 in TURNED] + four_straight(0) + [wide for wide, narrow in beyond]
+        banks = [bank(i) for i in range(BANKS)]
+        opening = list(zip(banks, first))
+        early = len(TURNED) + START // P
+        for acc, (stationary, moving, leave) in opening[: len(TURNED)]:
+            multiply(acc, stationary, moving, 0, (0, START))
+        for acc, (stationary, moving, leave) in opening[len(TURNED) : early]:
+            multiply(acc, stationary, moving, 0)
+        for acc, (stationary, moving, leave) in opening[: len(TURNED)]:
+            multiply(acc, stationary, moving, 0, (START, WIDE))
+        for acc, (stationary, moving, leave) in opening[early:]:
+            multiply(acc, stationary, moving, 0)
+        for g in range(1, PASSES):
+            for acc, (stationary, moving, leave) in opening:
                 multiply(acc, stationary, moving, g)
-        for acc, (stationary, moving, leave) in zip(banks, first):
+        for acc, (stationary, moving, leave) in opening:
             leave(acc)
 
         load_piece(2)
 
-        later = []
+        later = [narrow for wide, narrow in beyond]
         for t0 in range(FIRST, LAST, WIDE):
-            later += chunk(t0)
+            later += four_straight(t0) + [turned(t0, e0) for e0 in TURNED]
         for t0 in range(LAST, T - P, P):
             later += whole_rows(t0)
         later += [straight(T - P, 0, WIDE)] + [straight(T - P, e0, e0 + P) for e0 in range(WIDE, E, P)]
         for i, (stationary, moving, leave) in enumerate(later):
-            acc = bank(len(first) + i)
+            acc = bank(i)
             for g in range(PASSES):
                 multiply(acc, stationary, moving, g)
             leave(acc)

@@ -24,12 +24,13 @@ LATER_PIECES = ((FIRST, FIRST + WIDE), (FIRST + WIDE, FIRST + 3 * WIDE), (FIRST 
 LAST = T - (T - FIRST) % WIDE
 START = WIDE // 2
 
-W_SCALE_RUNS = ((0, 2), (2, 4), (4, 8))
-X_SCALE_RUNS = ((0, 1), (1, 3), (3, 8))
+W_SCALE_RUNS = ((0, 2), (2, 4), (4, 6), (6, 8))
+X_SCALE_RUNS = ((0, 1), (1, 3), (3, 5), (5, 8))
 HALVES = ((0, PASSES // 2), (PASSES // 2, PASSES))
-LATER_CODE_RUNS = (HALVES, ((0, PASSES),), HALVES)
+LATER_CODE_RUNS = (HALVES, ((0, PASSES),), ((0, PASSES),))
 
-WARM_UPS = 6
+EARLY_PLANES = 3
+WARM_UPS = 5
 
 
 def tile_longcatrouter_kernel(tc, x_words, x_scales, w_words, w_scales, out):
@@ -90,7 +91,8 @@ def tile_longcatrouter_kernel(tc, x_words, x_scales, w_words, w_scales, out):
                 load_codes(codes, x_words)
 
         warm = keep.tile([P, P], BF16, name="warm")
-        for tile in (warm, w_stage[0], x_planes[0][0], x_planes[1][0]):
+        by_need = sorted(x_planes + w_planes[1:], key=lambda plane: plane[1])
+        for tile in [warm, w_stage[0]] + [plane[0] for plane in by_need[:EARLY_PLANES]]:
             zero(tile)
 
         load_codes(x_codes[0], x_words, (0, START))
@@ -103,15 +105,17 @@ def tile_longcatrouter_kernel(tc, x_words, x_scales, w_words, w_scales, out):
         load_codes(x_codes[0], x_words, (START, FIRST))
         nc.vector.tensor_copy(out=live_rows(x_planes[0][0], 0), in_=live_rows(x_stage[0], 0))
         nc.vector.tensor_copy(out=w_planes[0][0][:].bitcast(I32), in_=w_stage[0][:].bitcast(I32))
-        for plane in [w_planes[1], x_planes[2], w_planes[2]] + later_planes:
+        for plane in by_need[EARLY_PLANES:] + later_planes:
             zero(plane[0])
         for g in range(1, PASSES):
-            load_codes(w_codes[g], w_words)
             load_codes(x_codes[g], x_words)
+            load_codes(w_codes[g], w_words, (WIDE, E) if g == 1 else (0, E))
             for planes, scales in ((w_planes, w_scales), (x_planes, x_scales)):
                 for plane in planes:
                     if plane[1] == g:
                         load_scales(plane, scales)
+            if g == 1:
+                load_codes(w_codes[g], w_words, (0, WIDE))
         load_piece(0)
         load_piece(1)
 
@@ -210,7 +214,7 @@ def tile_longcatrouter_kernel(tc, x_words, x_scales, w_words, w_scales, out):
 
         later = [narrow for wide, narrow in beyond]
         for t0 in range(FIRST, LAST, WIDE):
-            later += four_straight(t0) + [turned(t0, e0) for e0 in TURNED]
+            later += [turned(t0, e0) for e0 in TURNED] + four_straight(t0)
         for t0 in range(LAST, T - P, P):
             later += whole_rows(t0)
         later += [straight(T - P, 0, WIDE)] + [straight(T - P, e0, e0 + P) for e0 in range(WIDE, E, P)]

@@ -26,8 +26,6 @@ START = WIDE // 2
 
 W_SCALE_RUNS = ((0, 2), (2, 4), (4, 6), (6, 8))
 X_SCALE_RUNS = ((0, 1), (1, 3), (3, 5), (5, 8))
-HALVES = ((0, PASSES // 2), (PASSES // 2, PASSES))
-LATER_CODE_RUNS = (HALVES, ((0, PASSES),), ((0, PASSES),))
 
 EARLY_PLANES = 3
 WARM_UPS = 5
@@ -52,10 +50,7 @@ def tile_longcatrouter_kernel(tc, x_words, x_scales, w_words, w_scales, out):
         x_codes = [part("x_codes", g, g + 1, 0, FIRST, WORD) for g in range(PASSES)]
         w_planes = [part("w_planes", g0, g1, 0, E, 1) for g0, g1 in W_SCALE_RUNS]
         x_planes = [part("x_planes", g0, g1, 0, FIRST, 1) for g0, g1 in X_SCALE_RUNS]
-        later_codes = [
-            [part("x_codes", g0, g1, t0, t1, WORD) for g0, g1 in runs]
-            for (t0, t1), runs in zip(LATER_PIECES, LATER_CODE_RUNS)
-        ]
+        later_codes = [part("x_codes", 0, PASSES, t0, t1, WORD) for t0, t1 in LATER_PIECES]
         later_planes = [part("x_planes", 0, PASSES, t0, t1, 1) for t0, t1 in LATER_PIECES]
         w_stage = part("w_stage", *W_SCALE_RUNS[0], 0, E, 1)
         x_stage = part("x_stage", *X_SCALE_RUNS[0], 0, FIRST, 1)
@@ -85,10 +80,8 @@ def tile_longcatrouter_kernel(tc, x_words, x_scales, w_words, w_scales, out):
             nc.sync.dma_start(out=live_rows(tile, quadrant), in_=src.bitcast(I32))
 
         def load_piece(i):
-            load_codes(later_codes[i][0], x_words)
+            load_codes(later_codes[i], x_words)
             load_scales(later_planes[i], x_scales)
-            for codes in later_codes[i][1:]:
-                load_codes(codes, x_words)
 
         warm = keep.tile([P, P], BF16, name="warm")
         by_need = sorted(x_planes + w_planes[1:], key=lambda plane: plane[1])
@@ -128,7 +121,7 @@ def tile_longcatrouter_kernel(tc, x_words, x_scales, w_words, w_scales, out):
             nc.tensor.matmul(warm_bank[:], warm[:], warm_columns, start=True, stop=True)
 
         def tokens(t0, t1):
-            return x_codes + sum(later_codes, []), x_planes + later_planes, t0, t1
+            return x_codes + later_codes, x_planes + later_planes, t0, t1
 
         def experts(e0, e1):
             return w_codes, w_planes, e0, e1
@@ -215,9 +208,9 @@ def tile_longcatrouter_kernel(tc, x_words, x_scales, w_words, w_scales, out):
         later = [narrow for wide, narrow in beyond]
         for t0 in range(FIRST, LAST, WIDE):
             later += [turned(t0, e0) for e0 in TURNED] + four_straight(t0)
-        for t0 in range(LAST, T - P, P):
-            later += whole_rows(t0)
-        later += [straight(T - P, 0, WIDE)] + [straight(T - P, e0, e0 + P) for e0 in range(WIDE, E, P)]
+        later += [straight(t0, 0, WIDE) for t0 in range(LAST, T, P)]
+        later += [straight(t0, WIDE, E) for t0 in range(LAST, T - P, P)]
+        later += [straight(T - P, e0, e0 + P) for e0 in TURNED]
         for i, (stationary, moving, leave) in enumerate(later):
             acc = bank(i)
             for g in range(PASSES):

@@ -27,7 +27,7 @@ START = WIDE // 2
 W_SCALE_RUNS = ((0, 2), (2, 4), (4, 6), (6, 8))
 X_SCALE_RUNS = ((0, 1), (1, 3), (3, 5), (5, 8))
 
-EARLY_PLANES = 3
+STAGED = (0, 2)
 WARM_UPS = 5
 
 
@@ -50,7 +50,8 @@ def tile_longcatrouter_kernel(tc, x_words, x_scales, w_words, w_scales, out):
         x_codes = [part("x_codes", g, g + 1, 0, FIRST, WORD) for g in range(PASSES)]
         w_planes = [part("w_planes", g0, g1, 0, E, 1) for g0, g1 in W_SCALE_RUNS]
         x_planes = [part("x_planes", g0, g1, 0, FIRST, 1) for g0, g1 in X_SCALE_RUNS]
-        later_codes = [part("x_codes", 0, PASSES, t0, t1, WORD) for t0, t1 in LATER_PIECES]
+        halves = ((0, PASSES // 2), (PASSES // 2, PASSES))
+        later_codes = [part("x_codes", g0, g1, t0, t1, WORD) for t0, t1 in LATER_PIECES for g0, g1 in halves]
         later_planes = [part("x_planes", 0, PASSES, t0, t1, 1) for t0, t1 in LATER_PIECES]
         w_stage = part("w_stage", *W_SCALE_RUNS[0], 0, E, 1)
         x_stage = part("x_stage", *X_SCALE_RUNS[0], 0, FIRST, 1)
@@ -58,12 +59,12 @@ def tile_longcatrouter_kernel(tc, x_words, x_scales, w_words, w_scales, out):
         def zero(tile):
             nc.vector.memset(tile[:].bitcast(I32), 0)
 
-        def load_codes(codes, words, columns=None):
+        def load_codes(codes, words, columns=None, queue=nc.sync):
             tile, g0, g1, first, end = codes
             c0, c1 = columns or (first, end)
             src = words[g0:g1, :, WORD * c0 : WORD * c1].rearrange("g p n -> p g n")
             dst = tile[:, :, WORD * (c0 - first) : WORD * (c1 - first)]
-            nc.sync.dma_start(out=dst.bitcast(I32), in_=src.bitcast(I32))
+            queue.dma_start(out=dst.bitcast(I32), in_=src.bitcast(I32))
 
         def load_scales(plane, scales):
             tile, g0, g1, c0, c1 = plane
@@ -79,36 +80,40 @@ def tile_longcatrouter_kernel(tc, x_words, x_scales, w_words, w_scales, out):
             src = scales[g0:g1, 4 * quadrant : 4 * quadrant + 4, c0:c1].rearrange("g r n -> r g n")
             nc.sync.dma_start(out=live_rows(tile, quadrant), in_=src.bitcast(I32))
 
+        def move_rows(quadrant):
+            nc.vector.tensor_copy(out=live_rows(x_planes[0][0], quadrant), in_=live_rows(x_stage[0], quadrant))
+
         def load_piece(i):
-            load_codes(later_codes[i], x_words)
+            for codes in later_codes[len(halves) * i : len(halves) * (i + 1)]:
+                load_codes(codes, x_words)
             load_scales(later_planes[i], x_scales)
 
         warm = keep.tile([P, P], BF16, name="warm")
         by_need = sorted(x_planes + w_planes[1:], key=lambda plane: plane[1])
-        for tile in [warm, w_stage[0]] + [plane[0] for plane in by_need[:EARLY_PLANES]]:
+        for tile in (warm, w_stage[0], by_need[0][0]):
             zero(tile)
 
+        load_codes(w_codes[0], w_words, queue=nc.gpsimd)
         load_codes(x_codes[0], x_words, (0, START))
-        load_codes(w_codes[0], w_words, (WIDE, E))
-        load_quadrant(x_stage, x_scales, 0)
+        for quadrant in STAGED:
+            load_quadrant(x_stage, x_scales, quadrant)
         load_scales(w_stage, w_scales)
-        for quadrant in (2, 1, 3):
+        for quadrant in (1, 3):
             load_quadrant(x_planes[0], x_scales, quadrant)
-        load_codes(w_codes[0], w_words, (0, WIDE))
         load_codes(x_codes[0], x_words, (START, FIRST))
-        nc.vector.tensor_copy(out=live_rows(x_planes[0][0], 0), in_=live_rows(x_stage[0], 0))
+        move_rows(STAGED[0])
+        zero(by_need[1][0])
+        move_rows(STAGED[1])
         nc.vector.tensor_copy(out=w_planes[0][0][:].bitcast(I32), in_=w_stage[0][:].bitcast(I32))
-        for plane in by_need[EARLY_PLANES:] + later_planes:
+        for plane in by_need[2:] + later_planes:
             zero(plane[0])
         for g in range(1, PASSES):
             load_codes(x_codes[g], x_words)
-            load_codes(w_codes[g], w_words, (WIDE, E) if g == 1 else (0, E))
+            load_codes(w_codes[g], w_words)
             for planes, scales in ((w_planes, w_scales), (x_planes, x_scales)):
                 for plane in planes:
                     if plane[1] == g:
                         load_scales(plane, scales)
-            if g == 1:
-                load_codes(w_codes[g], w_words, (0, WIDE))
         load_piece(0)
         load_piece(1)
 
@@ -126,15 +131,15 @@ def tile_longcatrouter_kernel(tc, x_words, x_scales, w_words, w_scales, out):
         def experts(e0, e1):
             return w_codes, w_planes, e0, e1
 
-        def multiply(acc, stationary, moving, g, columns=None):
-            c0, c1 = columns or moving[2:]
+        def multiply(acc, stationary, moving, g):
+            c0, c1 = moving[2:]
             nc.tensor.matmul_mx(
-                out=acc[:, c0 - moving[2] : c1 - moving[2]],
+                out=acc[:, 0 : c1 - c0],
                 lhsT=window(stationary[0], g, *stationary[2:], WORD).bitcast(FP4X4),
                 lhsT_scale=window(stationary[1], g, *stationary[2:], 1),
                 rhs=window(moving[0], g, c0, c1, WORD).bitcast(FP4X4),
                 rhs_scale=window(moving[1], g, c0, c1, 1),
-                start=(g == 0 and c0 == moving[2]),
+                start=(g == 0),
                 stop=(g == PASSES - 1),
             )
 
@@ -185,19 +190,10 @@ def tile_longcatrouter_kernel(tc, x_words, x_scales, w_words, w_scales, out):
             return [group(i) for i in range(WIDE // P)]
 
         beyond = [whole_rows(t0) for t0 in range(WIDE, FIRST, P)]
-        first = [turned(0, e0) for e0 in TURNED] + four_straight(0) + [wide for wide, narrow in beyond]
+        first = four_straight(0) + [turned(0, e0) for e0 in TURNED] + [wide for wide, narrow in beyond]
         banks = [bank(i) for i in range(BANKS)]
         opening = list(zip(banks, first))
-        early = len(TURNED) + START // P
-        for acc, (stationary, moving, leave) in opening[: len(TURNED)]:
-            multiply(acc, stationary, moving, 0, (0, START))
-        for acc, (stationary, moving, leave) in opening[len(TURNED) : early]:
-            multiply(acc, stationary, moving, 0)
-        for acc, (stationary, moving, leave) in opening[: len(TURNED)]:
-            multiply(acc, stationary, moving, 0, (START, WIDE))
-        for acc, (stationary, moving, leave) in opening[early:]:
-            multiply(acc, stationary, moving, 0)
-        for g in range(1, PASSES):
+        for g in range(PASSES):
             for acc, (stationary, moving, leave) in opening:
                 multiply(acc, stationary, moving, g)
         for acc, (stationary, moving, leave) in opening:

@@ -28,6 +28,7 @@ W_SCALE_RUNS = ((0, 2), (2, 4), (4, 6), (6, 8))
 X_SCALE_RUNS = ((0, 1), (1, 3), (3, 5), (5, 8))
 
 STAGED = (0, 2)
+EARLY_PLANES = 3
 WARM_UPS = 5
 
 
@@ -50,21 +51,24 @@ def tile_longcatrouter_kernel(tc, x_words, x_scales, w_words, w_scales, out):
         x_codes = [part("x_codes", g, g + 1, 0, FIRST, WORD) for g in range(PASSES)]
         w_planes = [part("w_planes", g0, g1, 0, E, 1) for g0, g1 in W_SCALE_RUNS]
         x_planes = [part("x_planes", g0, g1, 0, FIRST, 1) for g0, g1 in X_SCALE_RUNS]
-        halves = ((0, PASSES // 2), (PASSES // 2, PASSES))
-        later_codes = [part("x_codes", g0, g1, t0, t1, WORD) for t0, t1 in LATER_PIECES for g0, g1 in halves]
+        later_codes = []
+        for t0, t1 in LATER_PIECES:
+            step = PASSES if t1 - t0 <= WIDE else PASSES // 2
+            later_codes += [part("x_codes", g, g + step, t0, t1, WORD) for g in range(0, PASSES, step)]
         later_planes = [part("x_planes", 0, PASSES, t0, t1, 1) for t0, t1 in LATER_PIECES]
         w_stage = part("w_stage", *W_SCALE_RUNS[0], 0, E, 1)
         x_stage = part("x_stage", *X_SCALE_RUNS[0], 0, FIRST, 1)
+        codes_stage = part("codes_stage", 0, 1, 0, START, WORD)
 
         def zero(tile):
             nc.vector.memset(tile[:].bitcast(I32), 0)
 
-        def load_codes(codes, words, columns=None, queue=nc.sync):
+        def load_codes(codes, words, columns=None):
             tile, g0, g1, first, end = codes
             c0, c1 = columns or (first, end)
             src = words[g0:g1, :, WORD * c0 : WORD * c1].rearrange("g p n -> p g n")
             dst = tile[:, :, WORD * (c0 - first) : WORD * (c1 - first)]
-            queue.dma_start(out=dst.bitcast(I32), in_=src.bitcast(I32))
+            nc.sync.dma_start(out=dst.bitcast(I32), in_=src.bitcast(I32))
 
         def load_scales(plane, scales):
             tile, g0, g1, c0, c1 = plane
@@ -80,32 +84,30 @@ def tile_longcatrouter_kernel(tc, x_words, x_scales, w_words, w_scales, out):
             src = scales[g0:g1, 4 * quadrant : 4 * quadrant + 4, c0:c1].rearrange("g r n -> r g n")
             nc.sync.dma_start(out=live_rows(tile, quadrant), in_=src.bitcast(I32))
 
-        def move_rows(quadrant):
-            nc.vector.tensor_copy(out=live_rows(x_planes[0][0], quadrant), in_=live_rows(x_stage[0], quadrant))
-
         def load_piece(i):
-            for codes in later_codes[len(halves) * i : len(halves) * (i + 1)]:
-                load_codes(codes, x_words)
+            for codes in later_codes:
+                if codes[3:] == LATER_PIECES[i]:
+                    load_codes(codes, x_words)
             load_scales(later_planes[i], x_scales)
 
         warm = keep.tile([P, P], BF16, name="warm")
         by_need = sorted(x_planes + w_planes[1:], key=lambda plane: plane[1])
-        for tile in (warm, w_stage[0], by_need[0][0]):
+        for tile in [warm, w_stage[0]] + [plane[0] for plane in by_need[:EARLY_PLANES]]:
             zero(tile)
 
-        load_codes(w_codes[0], w_words, queue=nc.gpsimd)
-        load_codes(x_codes[0], x_words, (0, START))
         for quadrant in STAGED:
             load_quadrant(x_stage, x_scales, quadrant)
+        load_codes(codes_stage, x_words)
         load_scales(w_stage, w_scales)
+        load_codes(w_codes[0], w_words)
         for quadrant in (1, 3):
             load_quadrant(x_planes[0], x_scales, quadrant)
         load_codes(x_codes[0], x_words, (START, FIRST))
-        move_rows(STAGED[0])
-        zero(by_need[1][0])
-        move_rows(STAGED[1])
+        for quadrant in STAGED:
+            nc.vector.tensor_copy(out=live_rows(x_planes[0][0], quadrant), in_=live_rows(x_stage[0], quadrant))
+        nc.vector.tensor_copy(out=x_codes[0][0][:, :, 0 : WORD * START].bitcast(I32), in_=codes_stage[0][:].bitcast(I32))
         nc.vector.tensor_copy(out=w_planes[0][0][:].bitcast(I32), in_=w_stage[0][:].bitcast(I32))
-        for plane in by_need[2:] + later_planes:
+        for plane in by_need[EARLY_PLANES:] + later_planes:
             zero(plane[0])
         for g in range(1, PASSES):
             load_codes(x_codes[g], x_words)
@@ -131,15 +133,15 @@ def tile_longcatrouter_kernel(tc, x_words, x_scales, w_words, w_scales, out):
         def experts(e0, e1):
             return w_codes, w_planes, e0, e1
 
-        def multiply(acc, stationary, moving, g):
-            c0, c1 = moving[2:]
+        def multiply(acc, stationary, moving, g, columns=None):
+            c0, c1 = columns or moving[2:]
             nc.tensor.matmul_mx(
-                out=acc[:, 0 : c1 - c0],
+                out=acc[:, c0 - moving[2] : c1 - moving[2]],
                 lhsT=window(stationary[0], g, *stationary[2:], WORD).bitcast(FP4X4),
                 lhsT_scale=window(stationary[1], g, *stationary[2:], 1),
                 rhs=window(moving[0], g, c0, c1, WORD).bitcast(FP4X4),
                 rhs_scale=window(moving[1], g, c0, c1, 1),
-                start=(g == 0),
+                start=(g == 0 and c0 == moving[2]),
                 stop=(g == PASSES - 1),
             )
 
@@ -190,10 +192,19 @@ def tile_longcatrouter_kernel(tc, x_words, x_scales, w_words, w_scales, out):
             return [group(i) for i in range(WIDE // P)]
 
         beyond = [whole_rows(t0) for t0 in range(WIDE, FIRST, P)]
-        first = four_straight(0) + [turned(0, e0) for e0 in TURNED] + [wide for wide, narrow in beyond]
+        first = [turned(0, e0) for e0 in TURNED] + four_straight(0) + [wide for wide, narrow in beyond]
         banks = [bank(i) for i in range(BANKS)]
         opening = list(zip(banks, first))
-        for g in range(PASSES):
+        early = len(TURNED) + START // P
+        for acc, (stationary, moving, leave) in opening[: len(TURNED)]:
+            multiply(acc, stationary, moving, 0, (0, START))
+        for acc, (stationary, moving, leave) in opening[len(TURNED) : early]:
+            multiply(acc, stationary, moving, 0)
+        for acc, (stationary, moving, leave) in opening[: len(TURNED)]:
+            multiply(acc, stationary, moving, 0, (START, WIDE))
+        for acc, (stationary, moving, leave) in opening[early:]:
+            multiply(acc, stationary, moving, 0)
+        for g in range(1, PASSES):
             for acc, (stationary, moving, leave) in opening:
                 multiply(acc, stationary, moving, g)
         for acc, (stationary, moving, leave) in opening:

@@ -51,10 +51,7 @@ def tile_longcatrouter_kernel(tc, x_words, x_scales, w_words, w_scales, out):
         x_codes = [part("x_codes", g, g + 1, 0, FIRST, WORD) for g in range(PASSES)]
         w_planes = [part("w_planes", g0, g1, 0, E, 1) for g0, g1 in W_SCALE_RUNS]
         x_planes = [part("x_planes", g0, g1, 0, FIRST, 1) for g0, g1 in X_SCALE_RUNS]
-        later_codes = []
-        for t0, t1 in LATER_PIECES:
-            step = PASSES if t1 - t0 <= WIDE else PASSES // 2
-            later_codes += [part("x_codes", g, g + step, t0, t1, WORD) for g in range(0, PASSES, step)]
+        later_codes = [part("x_codes", 0, PASSES, t0, t1, WORD) for t0, t1 in LATER_PIECES]
         later_planes = [part("x_planes", 0, PASSES, t0, t1, 1) for t0, t1 in LATER_PIECES]
         w_stage = part("w_stage", *W_SCALE_RUNS[0], 0, E, 1)
         x_stage = part("x_stage", *X_SCALE_RUNS[0], 0, FIRST, 1)
@@ -85,9 +82,7 @@ def tile_longcatrouter_kernel(tc, x_words, x_scales, w_words, w_scales, out):
             nc.sync.dma_start(out=live_rows(tile, quadrant), in_=src.bitcast(I32))
 
         def load_piece(i):
-            for codes in later_codes:
-                if codes[3:] == LATER_PIECES[i]:
-                    load_codes(codes, x_words)
+            load_codes(later_codes[i], x_words)
             load_scales(later_planes[i], x_scales)
 
         warm = keep.tile([P, P], BF16, name="warm")
@@ -110,12 +105,15 @@ def tile_longcatrouter_kernel(tc, x_words, x_scales, w_words, w_scales, out):
         for plane in by_need[EARLY_PLANES:] + later_planes:
             zero(plane[0])
         for g in range(1, PASSES):
-            load_codes(x_codes[g], x_words)
-            load_codes(w_codes[g], w_words)
+            load_codes(x_codes[g], x_words, (0, START) if g == 1 else (0, FIRST))
+            load_codes(w_codes[g], w_words, (WIDE, E) if g == 1 else (0, E))
             for planes, scales in ((w_planes, w_scales), (x_planes, x_scales)):
                 for plane in planes:
                     if plane[1] == g:
                         load_scales(plane, scales)
+            if g == 1:
+                load_codes(w_codes[g], w_words, (0, WIDE))
+                load_codes(x_codes[g], x_words, (START, FIRST))
         load_piece(0)
         load_piece(1)
 
@@ -196,15 +194,16 @@ def tile_longcatrouter_kernel(tc, x_words, x_scales, w_words, w_scales, out):
         banks = [bank(i) for i in range(BANKS)]
         opening = list(zip(banks, first))
         early = len(TURNED) + START // P
-        for acc, (stationary, moving, leave) in opening[: len(TURNED)]:
-            multiply(acc, stationary, moving, 0, (0, START))
-        for acc, (stationary, moving, leave) in opening[len(TURNED) : early]:
-            multiply(acc, stationary, moving, 0)
-        for acc, (stationary, moving, leave) in opening[: len(TURNED)]:
-            multiply(acc, stationary, moving, 0, (START, WIDE))
-        for acc, (stationary, moving, leave) in opening[early:]:
-            multiply(acc, stationary, moving, 0)
-        for g in range(1, PASSES):
+        for g in (0, 1):
+            for acc, (stationary, moving, leave) in opening[: len(TURNED)]:
+                multiply(acc, stationary, moving, g, (0, START))
+            for acc, (stationary, moving, leave) in opening[len(TURNED) : early]:
+                multiply(acc, stationary, moving, g)
+            for acc, (stationary, moving, leave) in opening[: len(TURNED)]:
+                multiply(acc, stationary, moving, g, (START, WIDE))
+            for acc, (stationary, moving, leave) in opening[early:]:
+                multiply(acc, stationary, moving, g)
+        for g in range(2, PASSES):
             for acc, (stationary, moving, leave) in opening:
                 multiply(acc, stationary, moving, g)
         for acc, (stationary, moving, leave) in opening:

@@ -24,12 +24,8 @@ LATER_PIECES = ((FIRST, FIRST + WIDE), (FIRST + WIDE, FIRST + 3 * WIDE), (FIRST 
 LAST = T - (T - FIRST) % WIDE
 START = WIDE // 2
 
-W_SCALE_RUNS = ((0, 2), (2, 4), (4, 6), (6, 8))
-X_SCALE_RUNS = ((0, 1), (1, 3), (3, 5), (5, 8))
-
-STAGED = (0, 2)
-EARLY_PLANES = 3
-WARM_UPS = 5
+HALVES = (0, 2)
+WARM_UPS = 3
 
 
 def tile_longcatrouter_kernel(tc, x_words, x_scales, w_words, w_scales, out):
@@ -47,18 +43,15 @@ def tile_longcatrouter_kernel(tc, x_words, x_scales, w_words, w_scales, out):
             tile, g0, g1, first, end = [x for x in parts if x[1] <= g < x[2] and x[3] <= c0 < x[4]][0]
             return tile[:, g - g0, width * (c0 - first) : width * (c1 - first)]
 
+        def staged_plane(name, g, c1):
+            return keep.tile([P, 2, c1], U8, align_bytes=256, name="%s_%d" % (name, g)), g, g + 1, 0, c1
+
         w_codes = [part("w_codes", g, g + 1, 0, E, WORD) for g in range(PASSES)]
         x_codes = [part("x_codes", g, g + 1, 0, FIRST, WORD) for g in range(PASSES)]
-        w_planes = [part("w_planes", g0, g1, 0, E, 1) for g0, g1 in W_SCALE_RUNS]
-        x_planes = [part("x_planes", g0, g1, 0, FIRST, 1) for g0, g1 in X_SCALE_RUNS]
+        w_planes = [staged_plane("w_plane", g, E) for g in range(PASSES)]
+        x_planes = [staged_plane("x_plane", g, FIRST) for g in range(PASSES)]
         later_codes = [part("x_codes", 0, PASSES, t0, t1, WORD) for t0, t1 in LATER_PIECES]
         later_planes = [part("x_planes", 0, PASSES, t0, t1, 1) for t0, t1 in LATER_PIECES]
-        w_stage = part("w_stage", *W_SCALE_RUNS[0], 0, E, 1)
-        x_stage = part("x_stage", *X_SCALE_RUNS[0], 0, FIRST, 1)
-        codes_stage = part("codes_stage", 0, 1, 0, START, WORD)
-
-        def zero(tile):
-            nc.vector.memset(tile[:].bitcast(I32), 0)
 
         def load_codes(codes, words, columns=None):
             tile, g0, g1, first, end = codes
@@ -73,47 +66,38 @@ def tile_longcatrouter_kernel(tc, x_words, x_scales, w_words, w_scales, out):
                 src = scales[g0:g1, r:16:4, c0:c1].rearrange("g q n -> q g n")
                 nc.sync.dma_start(out=tile[r:P:QUAD, :, :].bitcast(I32), in_=src.bitcast(I32))
 
-        def live_rows(tile, quadrant):
-            return tile[QUAD * quadrant : QUAD * quadrant + 4].bitcast(I32)
+        def load_half(plane, scales, quadrant):
+            tile, g, g1, c0, c1 = plane
+            src = scales[g, 4 * quadrant : 4 * quadrant + 8, c0:c1].rearrange("(s r) n -> r s n", r=4)
+            nc.sync.dma_start(out=tile[QUAD * quadrant : QUAD * quadrant + 4].bitcast(I32), in_=src.bitcast(I32))
 
-        def load_quadrant(plane, scales, quadrant):
-            tile, g0, g1, c0, c1 = plane
-            src = scales[g0:g1, 4 * quadrant : 4 * quadrant + 4, c0:c1].rearrange("g r n -> r g n")
-            nc.sync.dma_start(out=live_rows(tile, quadrant), in_=src.bitcast(I32))
+        def move_half(plane, quadrant):
+            p0 = QUAD * quadrant
+            src, dst = plane[0][p0 : p0 + 4, 1, :], plane[0][p0 + QUAD : p0 + QUAD + 4, 0, :]
+            nc.vector.tensor_copy(out=dst.bitcast(I32), in_=src.bitcast(I32))
 
         def load_piece(i):
             load_codes(later_codes[i], x_words)
             load_scales(later_planes[i], x_scales)
 
         warm = keep.tile([P, P], BF16, name="warm")
-        by_need = sorted(x_planes + w_planes[1:], key=lambda plane: plane[1])
-        for tile in [warm, w_stage[0]] + [plane[0] for plane in by_need[:EARLY_PLANES]]:
-            zero(tile)
+        nc.vector.memset(warm[:].bitcast(I32), 0)
 
-        for quadrant in STAGED:
-            load_quadrant(x_stage, x_scales, quadrant)
-        load_codes(codes_stage, x_words)
-        load_scales(w_stage, w_scales)
-        load_codes(w_codes[0], w_words)
-        for quadrant in (1, 3):
-            load_quadrant(x_planes[0], x_scales, quadrant)
-        load_codes(x_codes[0], x_words, (START, FIRST))
-        for quadrant in STAGED:
-            nc.vector.tensor_copy(out=live_rows(x_planes[0][0], quadrant), in_=live_rows(x_stage[0], quadrant))
-        nc.vector.tensor_copy(out=x_codes[0][0][:, :, 0 : WORD * START].bitcast(I32), in_=codes_stage[0][:].bitcast(I32))
-        nc.vector.tensor_copy(out=w_planes[0][0][:].bitcast(I32), in_=w_stage[0][:].bitcast(I32))
-        for plane in by_need[EARLY_PLANES:] + later_planes:
-            zero(plane[0])
-        for g in range(1, PASSES):
-            load_codes(x_codes[g], x_words, (0, START) if g == 1 else (0, FIRST))
-            load_codes(w_codes[g], w_words, (WIDE, E) if g == 1 else (0, E))
-            for planes, scales in ((w_planes, w_scales), (x_planes, x_scales)):
-                for plane in planes:
-                    if plane[1] == g:
-                        load_scales(plane, scales)
-            if g == 1:
+        for g in range(PASSES):
+            for quadrant in HALVES:
+                load_half(x_planes[g], x_scales, quadrant)
+                load_half(w_planes[g], w_scales, quadrant)
+            for quadrant in HALVES:
+                move_half(x_planes[g], quadrant)
+                move_half(w_planes[g], quadrant)
+            if g < 2:
+                load_codes(x_codes[g], x_words, (0, START))
+                load_codes(w_codes[g], w_words, (WIDE, E))
                 load_codes(w_codes[g], w_words, (0, WIDE))
                 load_codes(x_codes[g], x_words, (START, FIRST))
+            else:
+                load_codes(x_codes[g], x_words)
+                load_codes(w_codes[g], w_words)
         load_piece(0)
         load_piece(1)
 
@@ -162,18 +146,19 @@ def tile_longcatrouter_kernel(tc, x_words, x_scales, w_words, w_scales, out):
 
             return experts(e0, e0 + P), tokens(t0, t0 + WIDE), leave
 
-        def whole_rows(t0):
-            rows = keep.tile([P, E], F32, name="rows_%d" % t0)
+        def whole_rows(t0, blocks):
+            rows = keep.tile([P, blocks, E], F32, name="rows_%d" % t0)
 
-            def group(e0, e1):
+            def group(i, e0, e1):
                 def leave(acc):
-                    nc.vector.tensor_copy(out=rows[:, e0:e1], in_=acc[:, 0 : e1 - e0])
-                    if e1 == E:
-                        nc.sync.dma_start(out=out[t0 : t0 + P, :], in_=rows[:])
+                    nc.vector.tensor_copy(out=rows[:, i, e0:e1], in_=acc[:, 0 : e1 - e0])
+                    if e1 == E and i == blocks - 1:
+                        dst = out[t0 : t0 + P * blocks, :].rearrange("(i p) e -> p i e", p=P)
+                        nc.sync.dma_start(out=dst, in_=rows[:])
 
-                return tokens(t0, t0 + P), experts(e0, e1), leave
+                return tokens(t0 + P * i, t0 + P * (i + 1)), experts(e0, e1), leave
 
-            return [group(0, WIDE), group(WIDE, E)]
+            return [group(i, 0, WIDE) for i in range(blocks)], [group(i, WIDE, E) for i in range(blocks)]
 
         def four_straight(t0):
             rows = keep.tile([P, WIDE // P, WIDE], F32, name="four_%d" % t0)
@@ -189,8 +174,8 @@ def tile_longcatrouter_kernel(tc, x_words, x_scales, w_words, w_scales, out):
 
             return [group(i) for i in range(WIDE // P)]
 
-        beyond = [whole_rows(t0) for t0 in range(WIDE, FIRST, P)]
-        first = [turned(0, e0) for e0 in TURNED] + four_straight(0) + [wide for wide, narrow in beyond]
+        wide_beyond, narrow_beyond = whole_rows(WIDE, (FIRST - WIDE) // P)
+        first = [turned(0, e0) for e0 in TURNED] + four_straight(0) + wide_beyond
         banks = [bank(i) for i in range(BANKS)]
         opening = list(zip(banks, first))
         early = len(TURNED) + START // P
@@ -211,7 +196,7 @@ def tile_longcatrouter_kernel(tc, x_words, x_scales, w_words, w_scales, out):
 
         load_piece(2)
 
-        later = [narrow for wide, narrow in beyond]
+        later = list(narrow_beyond)
         for t0 in range(FIRST, LAST, WIDE):
             later += [turned(t0, e0) for e0 in TURNED] + four_straight(t0)
         later += [straight(t0, 0, WIDE) for t0 in range(LAST, T, P)]

@@ -24,7 +24,8 @@ LATER_PIECES = ((FIRST, FIRST + WIDE), (FIRST + WIDE, FIRST + 3 * WIDE), (FIRST 
 LAST = T - (T - FIRST) % WIDE
 START = WIDE // 2
 
-HALVES = (0, 2)
+LOWER, UPPER = 0, 2
+W_CODE_RUNS = [(g, g + 1) for g in range(PASSES - 2)] + [(PASSES - 2, PASSES)]
 WARM_UPS = 3
 
 
@@ -46,7 +47,7 @@ def tile_longcatrouter_kernel(tc, x_words, x_scales, w_words, w_scales, out):
         def staged_plane(name, g, c1):
             return keep.tile([P, 2, c1], U8, align_bytes=256, name="%s_%d" % (name, g)), g, g + 1, 0, c1
 
-        w_codes = [part("w_codes", g, g + 1, 0, E, WORD) for g in range(PASSES)]
+        w_codes = [part("w_codes", g0, g1, 0, E, WORD) for g0, g1 in W_CODE_RUNS]
         x_codes = [part("x_codes", g, g + 1, 0, FIRST, WORD) for g in range(PASSES)]
         w_planes = [staged_plane("w_plane", g, E) for g in range(PASSES)]
         x_planes = [staged_plane("x_plane", g, FIRST) for g in range(PASSES)]
@@ -71,9 +72,9 @@ def tile_longcatrouter_kernel(tc, x_words, x_scales, w_words, w_scales, out):
             src = scales[g, 4 * quadrant : 4 * quadrant + 8, c0:c1].rearrange("(s r) n -> r s n", r=4)
             nc.sync.dma_start(out=tile[QUAD * quadrant : QUAD * quadrant + 4].bitcast(I32), in_=src.bitcast(I32))
 
-        def move_half(plane, quadrant):
+        def move_half(plane, quadrant, c0, c1):
             p0 = QUAD * quadrant
-            src, dst = plane[0][p0 : p0 + 4, 1, :], plane[0][p0 + QUAD : p0 + QUAD + 4, 0, :]
+            src, dst = plane[0][p0 : p0 + 4, 1, c0:c1], plane[0][p0 + QUAD : p0 + QUAD + 4, 0, c0:c1]
             nc.vector.tensor_copy(out=dst.bitcast(I32), in_=src.bitcast(I32))
 
         def load_piece(i):
@@ -84,20 +85,28 @@ def tile_longcatrouter_kernel(tc, x_words, x_scales, w_words, w_scales, out):
         nc.vector.memset(warm[:].bitcast(I32), 0)
 
         for g in range(PASSES):
-            for quadrant in HALVES:
-                load_half(x_planes[g], x_scales, quadrant)
+            for quadrant in (LOWER, UPPER):
                 load_half(w_planes[g], w_scales, quadrant)
-            for quadrant in HALVES:
-                move_half(x_planes[g], quadrant)
-                move_half(w_planes[g], quadrant)
-            if g < 2:
+                load_half(x_planes[g], x_scales, quadrant)
+            for quadrant in (LOWER, UPPER):
+                move_half(w_planes[g], quadrant, 0, E)
+                move_half(x_planes[g], quadrant, 0, FIRST)
+            if g == 0:
+                load_codes(x_codes[g], x_words, (0, START))
+                load_codes(w_codes[g], w_words, (WIDE, E))
+                load_codes(x_codes[g], x_words, (START, WIDE))
+                load_codes(w_codes[g], w_words, (0, WIDE))
+                load_codes(x_codes[g], x_words, (WIDE, FIRST))
+            elif g == 1:
                 load_codes(x_codes[g], x_words, (0, START))
                 load_codes(w_codes[g], w_words, (WIDE, E))
                 load_codes(w_codes[g], w_words, (0, WIDE))
                 load_codes(x_codes[g], x_words, (START, FIRST))
             else:
                 load_codes(x_codes[g], x_words)
-                load_codes(w_codes[g], w_words)
+                for codes in w_codes:
+                    if codes[1] == g:
+                        load_codes(codes, w_words)
         load_piece(0)
         load_piece(1)
 
@@ -179,15 +188,19 @@ def tile_longcatrouter_kernel(tc, x_words, x_scales, w_words, w_scales, out):
         banks = [bank(i) for i in range(BANKS)]
         opening = list(zip(banks, first))
         early = len(TURNED) + START // P
-        for g in (0, 1):
+        for columns in ((0, START), (START, WIDE)):
             for acc, (stationary, moving, leave) in opening[: len(TURNED)]:
-                multiply(acc, stationary, moving, g, (0, START))
-            for acc, (stationary, moving, leave) in opening[len(TURNED) : early]:
-                multiply(acc, stationary, moving, g)
-            for acc, (stationary, moving, leave) in opening[: len(TURNED)]:
-                multiply(acc, stationary, moving, g, (START, WIDE))
-            for acc, (stationary, moving, leave) in opening[early:]:
-                multiply(acc, stationary, moving, g)
+                multiply(acc, stationary, moving, 0, columns)
+        for acc, (stationary, moving, leave) in opening[len(TURNED) :]:
+            multiply(acc, stationary, moving, 0)
+        for acc, (stationary, moving, leave) in opening[: len(TURNED)]:
+            multiply(acc, stationary, moving, 1, (0, START))
+        for acc, (stationary, moving, leave) in opening[len(TURNED) : early]:
+            multiply(acc, stationary, moving, 1)
+        for acc, (stationary, moving, leave) in opening[: len(TURNED)]:
+            multiply(acc, stationary, moving, 1, (START, WIDE))
+        for acc, (stationary, moving, leave) in opening[early:]:
+            multiply(acc, stationary, moving, 1)
         for g in range(2, PASSES):
             for acc, (stationary, moving, leave) in opening:
                 multiply(acc, stationary, moving, g)

from contextlib import ExitStack

import concourse.mybir as mybir

T, D, E = 4096, 4096, 768
FLOPS = 2 * T * D * E

F32 = mybir.dt.float32
BF16 = mybir.dt.bfloat16
I32 = mybir.dt.int32
U8 = mybir.dt.uint8
FP4X4 = mybir.dt.float4_e2m1fn_x4

P = 128
QUAD = 32
PASSES = D // 512
BANKS = 8
WIDE = 512
WORD = 2
TURNED = range(WIDE, E, P)

FIRST = (BANKS - len(TURNED)) * P
LATER_PIECES = ((FIRST, FIRST + WIDE), (FIRST + WIDE, FIRST + 3 * WIDE), (FIRST + 3 * WIDE, T))
LAST = T - (T - FIRST) % WIDE
START = WIDE // 2

LOWER, UPPER = 0, 2
W_CODE_RUNS = [(g, g + 1) for g in range(PASSES - 2)] + [(PASSES - 2, PASSES)]
WARM_UPS = 3


def tile_longcatrouter_kernel(tc, x_words, x_scales, w_words, w_scales, out):
    nc = tc.nc
    with ExitStack() as ctx:
        keep = ctx.enter_context(tc.tile_pool(name="keep", bufs=1))
        psum = ctx.enter_context(tc.psum_pool(name="psum", bufs=1))
        ctx.enter_context(tc.manual_schedule())

        def part(name, g0, g1, c0, c1, width):
            shape = [P, g1 - g0, width * (c1 - c0)]
            return keep.tile(shape, U8, align_bytes=256, name="%s_%d_%d" % (name, g0, c0)), g0, g1, c0, c1

        def window(parts, g, c0, c1, width):
            tile, g0, g1, first, end = [x for x in parts if x[1] <= g < x[2] and x[3] <= c0 < x[4]][0]
            return tile[:, g - g0, width * (c0 - first) : width * (c1 - first)]

        def staged_plane(name, g, c1):
            return keep.tile([P, 2, c1], U8, align_bytes=256, name="%s_%d" % (name, g)), g, g + 1, 0, c1

        w_codes = [part("w_codes", g0, g1, 0, E, WORD) for g0, g1 in W_CODE_RUNS]
        x_codes = [part("x_codes", g, g + 1, 0, FIRST, WORD) for g in range(PASSES)]
        w_planes = [staged_plane("w_plane", g, E) for g in range(PASSES)]
        x_planes = [staged_plane("x_plane", g, FIRST) for g in range(PASSES)]
        later_codes = [part("x_codes", 0, PASSES, t0, t1, WORD) for t0, t1 in LATER_PIECES]
        later_planes = [part("x_planes", 0, PASSES, t0, t1, 1) for t0, t1 in LATER_PIECES]

        def load_codes(codes, words, columns=None):
            tile, g0, g1, first, end = codes
            c0, c1 = columns or (first, end)
            src = words[g0:g1, :, WORD * c0 : WORD * c1].rearrange("g p n -> p g n")
            dst = tile[:, :, WORD * (c0 - first) : WORD * (c1 - first)]
            nc.sync.dma_start(out=dst.bitcast(I32), in_=src.bitcast(I32))

        def load_scales(plane, scales):
            tile, g0, g1, c0, c1 = plane
            for r in range(4):
                src = scales[g0:g1, r:16:4, c0:c1].rearrange("g q n -> q g n")
                nc.sync.dma_start(out=tile[r:P:QUAD, :, :].bitcast(I32), in_=src.bitcast(I32))

        def load_half(plane, scales, quadrant):
            tile, g, g1, c0, c1 = plane
            src = scales[g, 4 * quadrant : 4 * quadrant + 8, c0:c1].rearrange("(s r) n -> r s n", r=4)
            nc.sync.dma_start(out=tile[QUAD * quadrant : QUAD * quadrant + 4].bitcast(I32), in_=src.bitcast(I32))

        def move_half(plane, quadrant, c0, c1):
            p0 = QUAD * quadrant
            src, dst = plane[0][p0 : p0 + 4, 1, c0:c1], plane[0][p0 + QUAD : p0 + QUAD + 4, 0, c0:c1]
            nc.vector.tensor_copy(out=dst.bitcast(I32), in_=src.bitcast(I32))

        def load_piece(i):
            load_codes(later_codes[i], x_words)
            load_scales(later_planes[i], x_scales)

        warm = keep.tile([P, P], BF16, name="warm")
        nc.vector.memset(warm[:].bitcast(I32), 0)

        for g in range(PASSES):
            for quadrant in (LOWER, UPPER):
                load_half(w_planes[g], w_scales, quadrant)
                load_half(x_planes[g], x_scales, quadrant)
            for quadrant in (LOWER, UPPER):
                move_half(w_planes[g], quadrant, 0, E)
                move_half(x_planes[g], quadrant, 0, FIRST)
            if g == 0:
                load_codes(x_codes[g], x_words, (0, START))
                load_codes(w_codes[g], w_words, (WIDE, E))
                load_codes(x_codes[g], x_words, (START, WIDE))
                load_codes(w_codes[g], w_words, (0, WIDE))
                load_codes(x_codes[g], x_words, (WIDE, FIRST))
            elif g == 1:
                load_codes(x_codes[g], x_words, (0, START))
                load_codes(w_codes[g], w_words, (WIDE, E))
                load_codes(w_codes[g], w_words, (0, WIDE))
                load_codes(x_codes[g], x_words, (START, FIRST))
            else:
                load_codes(x_codes[g], x_words)
                for codes in w_codes:
                    if codes[1] == g:
                        load_codes(codes, w_words)
        load_piece(0)
        load_piece(1)

        def bank(i):
            return psum.tile([P, WIDE], F32, tag="bank%d" % (i % BANKS), name="bank%d" % (i % BANKS))

        warm_bank = bank(BANKS - 1)
        warm_columns = warm[:].unsqueeze(1).to_broadcast([P, WIDE // P, P])
        for i in range(WARM_UPS):
            nc.tensor.matmul(warm_bank[:], warm[:], warm_columns, start=True, stop=True)

        def tokens(t0, t1):
            return x_codes + later_codes, x_planes + later_planes, t0, t1

        def experts(e0, e1):
            return w_codes, w_planes, e0, e1

        def multiply(acc, stationary, moving, g, columns=None):
            c0, c1 = columns or moving[2:]
            nc.tensor.matmul_mx(
                out=acc[:, c0 - moving[2] : c1 - moving[2]],
                lhsT=window(stationary[0], g, *stationary[2:], WORD).bitcast(FP4X4),
                lhsT_scale=window(stationary[1], g, *stationary[2:], 1),
                rhs=window(moving[0], g, c0, c1, WORD).bitcast(FP4X4),
                rhs_scale=window(moving[1], g, c0, c1, 1),
                start=(g == 0 and c0 == moving[2]),
                stop=(g == PASSES - 1),
            )

        def straight(t0, e0, e1):
            def leave(acc):
                logits = keep.tile([P, e1 - e0], F32, name="straight_%d_%d" % (t0, e0))
                nc.vector.tensor_copy(out=logits[:], in_=acc[:, 0 : e1 - e0])
                nc.sync.dma_start(out=out[t0 : t0 + P, e0:e1], in_=logits[:])

            return tokens(t0, t0 + P), experts(e0, e1), leave

        def turned(t0, e0):
            def leave(acc):
                logits = keep.tile([P, WIDE], F32, align_bytes=64, name="turned_%d_%d" % (t0, e0))
                nc.vector.transpose(out=logits[:], in_=acc[:])
                for i in range(P // QUAD):
                    dst = out[t0 : t0 + WIDE, e0 + QUAD * i : e0 + QUAD * (i + 1)].rearrange("(j a) b -> a j b", a=QUAD)
                    src = logits[QUAD * i : QUAD * (i + 1), :].rearrange("a (j b) -> a j b", b=QUAD)
                    nc.sync.dma_start(out=dst, in_=src)

            return experts(e0, e0 + P), tokens(t0, t0 + WIDE), leave

        def whole_rows(t0, blocks):
            rows = keep.tile([P, blocks, E], F32, name="rows_%d" % t0)

            def group(i, e0, e1):
                def leave(acc):
                    nc.vector.tensor_copy(out=rows[:, i, e0:e1], in_=acc[:, 0 : e1 - e0])
                    if e1 == E and i == blocks - 1:
                        dst = out[t0 : t0 + P * blocks, :].rearrange("(i p) e -> p i e", p=P)
                        nc.sync.dma_start(out=dst, in_=rows[:])

                return tokens(t0 + P * i, t0 + P * (i + 1)), experts(e0, e1), leave

            return [group(i, 0, WIDE) for i in range(blocks)], [group(i, WIDE, E) for i in range(blocks)]

        def four_straight(t0):
            rows = keep.tile([P, WIDE // P, WIDE], F32, name="four_%d" % t0)

            def group(i):
                def leave(acc):
                    nc.vector.tensor_copy(out=rows[:, i, :], in_=acc[:])
                    if i == WIDE // P - 1:
                        dst = out[t0 : t0 + WIDE, 0:WIDE].rearrange("(i p) e -> p i e", p=P)
                        nc.sync.dma_start(out=dst, in_=rows[:])

                return tokens(t0 + P * i, t0 + P * (i + 1)), experts(0, WIDE), leave

            return [group(i) for i in range(WIDE // P)]

        wide_beyond, narrow_beyond = whole_rows(WIDE, (FIRST - WIDE) // P)
        first = [turned(0, e0) for e0 in TURNED] + four_straight(0) + wide_beyond
        banks = [bank(i) for i in range(BANKS)]
        opening = list(zip(banks, first))
        early = len(TURNED) + START // P
        for columns in ((0, START), (START, WIDE)):
            for acc, (stationary, moving, leave) in opening[: len(TURNED)]:
                multiply(acc, stationary, moving, 0, columns)
        for acc, (stationary, moving, leave) in opening[len(TURNED) :]:
            multiply(acc, stationary, moving, 0)
        for acc, (stationary, moving, leave) in opening[: len(TURNED)]:
            multiply(acc, stationary, moving, 1, (0, START))
        for acc, (stationary, moving, leave) in opening[len(TURNED) : early]:
            multiply(acc, stationary, moving, 1)
        for acc, (stationary, moving, leave) in opening[: len(TURNED)]:
            multiply(acc, stationary, moving, 1, (START, WIDE))
        for acc, (stationary, moving, leave) in opening[early:]:
            multiply(acc, stationary, moving, 1)
        for g in range(2, PASSES):
            for acc, (stationary, moving, leave) in opening:
                multiply(acc, stationary, moving, g)
        for acc, (stationary, moving, leave) in opening:
            leave(acc)

        load_piece(2)

        later = list(narrow_beyond)
        for t0 in range(FIRST, LAST, WIDE):
            later += [turned(t0, e0) for e0 in TURNED] + four_straight(t0)
        later += [straight(t0, 0, WIDE) for t0 in range(LAST, T, P)]
        later += [straight(t0, WIDE, E) for t0 in range(LAST, T - P, P)]
        later += [straight(T - P, e0, e0 + P) for e0 in TURNED]
        for i, (stationary, moving, leave) in enumerate(later):
            acc = bank(i)
            for g in range(PASSES):
                multiply(acc, stationary, moving, g)
            leave(acc)
